import numpy as np
import ml_dtypes


def mxq(x, axis, fmt="e4m3"):
    dtype, down = {"e4m3": (ml_dtypes.float8_e4m3fn, 7), "e5m2": (ml_dtypes.float8_e5m2, 14)}[fmt]
    v = np.moveaxis(np.asarray(x, np.float32).astype(ml_dtypes.bfloat16).astype(np.float64), axis, -1)
    blocks = v.reshape(v.shape[:-1] + (-1, 32))
    amax = np.abs(blocks).max(-1, keepdims=True)
    byte = np.maximum(np.where(amax > 0, np.frexp(amax)[1] - 1 + 127, 0) - down, 1)
    scale = np.exp2(byte - 127.0)
    codes = (blocks / scale).astype(np.float32).astype(dtype).astype(np.float64)
    return np.moveaxis((codes * scale).reshape(v.shape), -1, axis)


WIDE = False


def mx_kscale(k):
    if not WIDE:
        return np.ones(k)
    levels = np.array([30, -30])
    if k % 512:
        return np.exp2(np.random.permutation(np.resize(levels, k // 32))).repeat(32)
    a = np.empty((k // 512, 16))
    for p in range(k // 512):
        a[p, :8] = np.random.permutation(np.resize(levels, 8))
        for g in range(8):
            far = levels[np.abs(levels - a[p, g]) >= 10]
            a[p, g + 8] = far[np.random.randint(len(far))]
    return np.exp2(a.ravel()).repeat(32)


BF16 = ml_dtypes.bfloat16


def bf(x):
    return np.asarray(x, np.float32).astype(BF16)


def f64(x):
    return np.asarray(x).astype(np.float64)


B, K, N = 1024, 1024, 1024


def setup_inputs():
    s = mx_kscale(K)
    s = s / s.max()
    return {"x": bf(np.random.standard_normal((B, K)) * s),
            "W": bf(np.random.standard_normal((K, N)) * 0.4 / np.sqrt(K) / s[:, None]),
            "P": bf(np.random.standard_normal(N) * 0.3),
            "w": bf(0.8 + 0.1 * np.random.standard_normal(1)),
            "p": bf(0.5 + 0.1 * np.random.standard_normal(1)),
            "sine_w": bf(1.2 + 0.1 * np.random.standard_normal(1)),
            "cosine_w": bf(-0.7 + 0.1 * np.random.standard_normal(1))}


def reference(x, W, P, w, p, sine_w, cosine_w):
    x = f64(x)
    original = f64(w) * x + f64(p)
    z = (mxq(x, 1, "e5m2") @ mxq(f64(W), 0, "e5m2")) + f64(P)
    periodic = f64(sine_w) * np.sin(z) + f64(cosine_w) * np.cos(z)
    return np.concatenate((original, periodic), axis=-1)

@@ -1,0 +1,277 @@
+import math
+from contextlib import ExitStack
+
+import concourse.mybir as mybir
+from concourse.masks import make_identity
+
+FLOPS = 2 * 1024 * 1024 * 1024
+
+F32 = mybir.dt.float32
+BF16 = mybir.dt.bfloat16
+I32 = mybir.dt.int32
+U32 = mybir.dt.uint32
+U8 = mybir.dt.uint8
+E5X4 = mybir.dt.float8_e5m2_x4
+ACT = mybir.ActivationFunctionType
+ALU = mybir.AluOpType
+
+P128 = 128
+NT = 8
+TWO_PI = 2.0 * math.pi
+INV_2PI = 1.0 / (2.0 * math.pi)
+GUESS = 0.68
+
+
+def tile_time2vec_kernel(tc, x, W, P, w, p, sine_w, cosine_w, out):
+    nc = tc.nc
+    with ExitStack() as ctx:
+        keep = ctx.enter_context(tc.tile_pool(name="keep", bufs=1))
+        work = ctx.enter_context(tc.tile_pool(name="work", bufs=3))
+        psum = ctx.enter_context(tc.psum_pool(name="psum", bufs=2))
+        ctx.enter_context(tc.manual_schedule())
+
+        bcs = keep.tile([P128, 64], BF16, name="bcs")
+        ones = keep.tile([P128, P128], BF16, name="ones")
+        mhalf = keep.tile([P128, 1], F32, name="mhalf")
+        mone = keep.tile([P128, 1], F32, name="mone")
+        bcp = keep.tile([P128, 1024], BF16, name="bcp")
+        ident = keep.tile([P128, P128], F32, name="ident")
+        nc.vector.memset(bcs[:], 0.0)
+        nc.vector.memset(mone[:], -1.0)
+        nc.vector.memset(ones[:], 1.0)
+        nc.vector.memset(mhalf[:], -0.5)
+        nc.vector.memset(bcp[:], 0.0)
+        make_identity(nc, ident[:])
+
+        for col, src in enumerate((sine_w, cosine_w, w, p)):
+            nc.scalar.dma_start(
+                out=bcs[0:1, 16 * col : 16 * col + 1], in_=src.rearrange("(a b) -> a b", a=1)
+            )
+        nc.scalar.dma_start(out=bcp[0:1, :], in_=P.rearrange("(a n) -> a n", a=1))
+
+        x_sb = [keep.tile([P128, 1024], BF16, name="x_sb%d" % i) for i in range(NT)]
+        w_raw = [[keep.tile([P128, 4, 512], BF16, name="w_raw%d%d" % (g, h)) for h in range(2)] for g in range(2)]
+
+        def load_x(i):
+            nc.sync.dma_start(out=x_sb[i][:], in_=x[128 * i : 128 * (i + 1), :])
+
+        def load_w(g, h):
+            nc.sync.dma_start(
+                out=w_raw[g][h][:],
+                in_=W[512 * g : 512 * (g + 1), 512 * h : 512 * (h + 1)].rearrange("(p j) n -> p j n", j=4),
+            )
+
+        load_w(0, 0)
+        load_x(0)
+        load_w(1, 0)
+        load_x(1)
+        load_w(0, 1)
+        load_x(2)
+        load_w(1, 1)
+        for i in range(3, NT):
+            load_x(i)
+
+        ks = keep.tile([P128, 16], F32, name="ks")
+        kg = keep.tile([P128, 16], F32, name="kg")
+        sc = keep.tile([P128, 4], F32, name="sc")
+
+        def kcol(t, j, n=1):
+            return t[:, j : j + n]
+
+        nc.scalar.activation(out=kcol(ks, 15), in_=mone[:], func=ACT.Sin)
+
+        ps_sc = psum.tile([P128, 64], F32, name="ps_sc", tag="xt", bufs=2)
+        nc.tensor.matmul(out=ps_sc[:], lhsT=ones[:], rhs=bcs[:], start=True, stop=True)
+        nc.vector.tensor_copy(out=sc[:], in_=ps_sc[:, 0:64:16])
+
+        swcw = sc[:, 0:2]
+        ab = kcol(ks, 0, 2)
+        nc.scalar.activation(out=ab, in_=swcw, func=ACT.Abs)
+        mx, rm, scn, t2, q, r, cs = kcol(kg, 0), kcol(kg, 1), kcol(kg, 2, 2), kcol(kg, 4, 2), kcol(kg, 6), kcol(kg, 7), kcol(kg, 8, 2)
+        c0, s0 = kcol(kg, 8), kcol(kg, 9)
+        gsg, hp, mm, phi0, g2, nc0 = kcol(kg, 10), kcol(kg, 11), kcol(kg, 12), kcol(kg, 13), kcol(kg, 14), kcol(kg, 15)
+        nc.gpsimd.tensor_scalar(out=mx, in0=kcol(ks, 0), scalar1=kcol(ks, 1), scalar2=1e-30, op0=ALU.max, op1=ALU.max)
+        nc.gpsimd.tensor_tensor(out=rm, in0=mx, in1=mone[:], op=ALU.pow)
+        nc.gpsimd.tensor_scalar(out=scn, in0=swcw, scalar1=rm, scalar2=None, op0=ALU.mult)
+        nc.gpsimd.tensor_tensor(out=t2, in0=scn, in1=scn, op=ALU.mult)
+        nc.gpsimd.tensor_scalar(out=q, in0=kcol(kg, 4), scalar1=kcol(kg, 5), scalar2=1e-30, op0=ALU.add, op1=ALU.max)
+        nc.gpsimd.tensor_tensor(out=r, in0=q, in1=mhalf[:], op=ALU.pow)
+        nc.gpsimd.tensor_scalar(out=cs, in0=scn, scalar1=r, scalar2=None, op0=ALU.mult)
+        nc.gpsimd.tensor_scalar(out=gsg, in0=s0, scalar1=0.0, scalar2=0.5, op0=ALU.is_ge, op1=ALU.subtract)
+        nc.gpsimd.tensor_scalar(out=hp, in0=c0, scalar1=-math.pi, scalar2=math.pi, op0=ALU.mult, op1=ALU.add)
+        nc.gpsimd.tensor_scalar(out=mm, in0=c0, scalar1=s0, scalar2=GUESS, op0=ALU.mult, op1=ALU.mult)
+        nc.gpsimd.tensor_scalar(out=phi0, in0=gsg, scalar1=hp, scalar2=mm, op0=ALU.mult, op1=ALU.add)
+        nc.gpsimd.tensor_scalar(out=g2, in0=gsg, scalar1=-2.0, scalar2=0.0, op0=ALU.mult, op1=ALU.add)
+        nc.gpsimd.tensor_scalar(out=nc0, in0=c0, scalar1=-1.0, scalar2=0.0, op0=ALU.mult, op1=ALU.add)
+
+        amp = kcol(ks, 14)
+        phi = kcol(ks, 13)
+
+        def phase_on_scalar():
+            cur = phi0
+            for it in range(2):
+                sn, cn, u = kcol(ks, 2 + 4 * it), kcol(ks, 3 + 4 * it), kcol(ks, 4 + 4 * it)
+                nxt = phi if it == 1 else kcol(ks, 5)
+                nc.scalar.activation(out=sn, in_=cur, func=ACT.Sin)
+                nc.scalar.activation(out=cn, in_=cur, func=ACT.Sin, bias=0.5 * math.pi, scale=g2)
+                nc.scalar.activation(out=u, in_=cn, func=ACT.Identity, bias=cur, scale=s0)
+                nc.scalar.activation(out=nxt, in_=sn, func=ACT.Identity, bias=u, scale=nc0)
+                cur = nxt
+            t = kcol(ks, 10)
+            nc.scalar.activation(out=t, in_=kcol(ks, 6), func=ACT.Copy, scale=sc[:, 1:2])
+            nc.scalar.activation(out=amp, in_=kcol(ks, 7), func=ACT.Identity, bias=t, scale=sc[:, 0:1])
+
+        wg = [[keep.tile([P128, 2048], BF16, name="wg%d%d" % (g, h), align_bytes=64) for h in range(2)] for g in range(2)]
+        wq = [[keep.tile([P128, 512], U32, name="wq%d%d" % (g, h), align_bytes=64) for h in range(2)] for g in range(2)]
+        ws = [[keep.tile([P128, 512], U8, name="ws%d%d" % (g, h), align_bytes=64) for h in range(2)] for g in range(2)]
+        pb = keep.tile([P128, 1024], F32, name="pb")
+        st = {}
+
+        def interleave_w(g, h):
+            nc.vector.tensor_copy(
+                out=wg[g][h][:].rearrange("p (n j) -> p n j", j=4),
+                in_=w_raw[g][h][:].rearrange("p j n -> p n j"),
+            )
+
+        def quantize_w(g, h):
+            nc.vector.quantize_mx(out=wq[g][h][:].bitcast(E5X4), scales=ws[g][h][:], in_=wg[g][h][:])
+
+        def transpose_x(i):
+            xt = psum.tile([P128, 512], F32, name="xt", tag="xt", bufs=2)
+            st["xt", i] = xt
+            words = x_sb[i][:].bitcast(F32)
+            for g in range(2):
+                for u in range(2):
+                    c = 2 * g + u
+                    nc.tensor.transpose(xt[:, 128 * c : 128 * (c + 1)], words[:, 256 * g + u : 256 * (g + 1) : 2], ident[:])
+
+        def copy_x(i):
+            xg = work.tile([P128, 1024], BF16, name="xg", tag="xg", bufs=3, align_bytes=64)
+            st["xg", i] = xg
+            nc.scalar.copy(
+                out=xg[:].bitcast(F32).rearrange("p (g r u) -> p g r u", g=2, u=2),
+                in_=st["xt", i][:].rearrange("p (g u r) -> p g r u", g=2, u=2),
+            )
+
+        def quantize_x(i):
+            xq = work.tile([P128, 256], U32, name="xq", tag="xq", bufs=3, align_bytes=64)
+            xs = work.tile([P128, 256], U8, name="xs", tag="xs", bufs=3, align_bytes=64)
+            st["xq", i] = xq
+            st["xs", i] = xs
+            nc.vector.quantize_mx(out=xq[:].bitcast(E5X4), scales=xs[:], in_=st["xg", i][:])
+
+        def matmuls(i):
+            for h in range(2):
+                acc = psum.tile([P128, 512], F32, name="acc", tag="acc", bufs=4)
+                st["acc", i, h] = acc
+                for g in range(2):
+                    nc.tensor.matmul_mx(
+                        out=acc[:],
+                        lhsT=st["xq", i][:, 128 * g : 128 * (g + 1)].bitcast(E5X4),
+                        lhsT_scale=st["xs", i][:, 128 * g : 128 * (g + 1)],
+                        rhs=wq[g][h][:].bitcast(E5X4),
+                        rhs_scale=ws[g][h][:],
+                        start=(g == 0),
+                        stop=(g == 1),
+                    )
+
+        def turns(i, h):
+            if h == 0:
+                st["v", i] = work.tile([P128, 1024], F32, name="v", tag="v", bufs=3)
+            nc.vector.scalar_tensor_tensor(
+                out=st["v", i][:, 512 * h : 512 * (h + 1)],
+                in0=st["acc", i, h][:],
+                scalar=INV_2PI,
+                in1=pb[:, 512 * h : 512 * (h + 1)],
+                op0=ALU.mult,
+                op1=ALU.add,
+            )
+
+        def whole_turns(i):
+            n = work.tile([P128, 1024], I32, name="n", tag="n", bufs=2)
+            st["n", i] = n
+            nc.vector.tensor_copy(out=n[:], in_=st["v", i][:])
+
+        def fraction(i):
+            f = work.tile([P128, 1024], F32, name="f", tag="f", bufs=2)
+            st["f", i] = f
+            nc.vector.tensor_tensor(out=f[:], in0=st["v", i][:], in1=st["n", i][:], op=ALU.subtract)
+
+        def sine(i):
+            s = work.tile([P128, 1024], F32, name="s", tag="s", bufs=2)
+            st["s", i] = s
+            nc.scalar.activation(out=s[:], in_=st["f", i][:], func=ACT.Sin, scale=TWO_PI)
+
+        def scale_store(i):
+            o = work.tile([P128, 1024], F32, name="o", tag="o", bufs=3)
+            nc.scalar.activation(out=o[:], in_=st["s", i][:], func=ACT.Copy, scale=amp)
+            nc.sync.dma_start(out=out[128 * i : 128 * (i + 1), 1024:2048], in_=o[:])
+
+        def linear(i):
+            lin = work.tile([P128, 1024], F32, name="lin", tag="lin", bufs=3)
+            nc.scalar.activation(out=lin[:], in_=x_sb[i][:], func=ACT.Identity, bias=sc[:, 3:4], scale=sc[:, 2:3])
+            nc.sync.dma_start(out=out[128 * i : 128 * (i + 1), 0:1024], in_=lin[:])
+
+        def bias_rows():
+            for h in range(2):
+                psp = psum.tile([P128, 512], F32, name="psp", tag="acc", bufs=4)
+                st["psp", h] = psp
+                nc.tensor.matmul(out=psp[:], lhsT=ones[:], rhs=bcp[:, 512 * h : 512 * (h + 1)], start=True, stop=True)
+
+        def bias_turns(h):
+            nc.vector.tensor_scalar(
+                out=pb[:, 512 * h : 512 * (h + 1)], in0=st["psp", h][:], scalar1=phi, scalar2=INV_2PI, op0=ALU.add, op1=ALU.mult
+            )
+
+        interleave_w(0, 0)
+        transpose_x(0)
+        copy_x(0)
+        linear(0)
+        interleave_w(1, 0)
+        transpose_x(1)
+        copy_x(1)
+        linear(1)
+        quantize_w(0, 0)
+        quantize_w(1, 0)
+        quantize_x(0)
+        phase_on_scalar()
+        bias_rows()
+        interleave_w(0, 1)
+        transpose_x(2)
+        copy_x(2)
+        linear(2)
+        interleave_w(1, 1)
+        quantize_x(1)
+        transpose_x(3)
+        copy_x(3)
+        linear(3)
+        quantize_w(0, 1)
+        quantize_w(1, 1)
+        bias_turns(0)
+        bias_turns(1)
+        quantize_x(2)
+        matmuls(0)
+        matmuls(1)
+
+        for i in range(NT + 1):
+            if i < NT:
+                turns(i, 0)
+                turns(i, 1)
+            if i >= 1:
+                fraction(i - 1)
+            if i < NT:
+                whole_turns(i)
+            if i + 3 < NT:
+                quantize_x(i + 3)
+            if i + 2 < NT:
+                matmuls(i + 2)
+            if i + 4 < NT:
+                transpose_x(i + 4)
+            if i >= 1:
+                sine(i - 1)
+            if i + 4 < NT:
+                copy_x(i + 4)
+            if i >= 1:
+                scale_store(i - 1)
+            if i + 4 < NT:
+                linear(i + 4)

@@ -20,6 +20,10 @@ NT = 8
 TWO_PI = 2.0 * math.pi
 INV_2PI = 1.0 / (2.0 * math.pi)
 GUESS = 0.68
+TINY = 1e-30
+GROUPS = ((0, 0), (1, 0), (0, 1), (1, 1))
+RUNS = (4, 4, 4, 2, 1, 1)
+PIECES = [(u, 0, 4) for u in range(15)] + [(15, 0, 2), (15, 2, 4)]
 
 
 def tile_time2vec_kernel(tc, x, W, P, w, p, sine_w, cosine_w, out):
@@ -27,27 +31,23 @@ def tile_time2vec_kernel(tc, x, W, P, w, p, sine_w, cosine_w, out):
     with ExitStack() as ctx:
         keep = ctx.enter_context(tc.tile_pool(name="keep", bufs=1))
         work = ctx.enter_context(tc.tile_pool(name="work", bufs=3))
-        psum = ctx.enter_context(tc.psum_pool(name="psum", bufs=2))
+        psum = ctx.enter_context(tc.psum_pool(name="psum", bufs=4))
         ctx.enter_context(tc.manual_schedule())
 
-        bcs = keep.tile([P128, 64], BF16, name="bcs")
-        ones = keep.tile([P128, P128], BF16, name="ones")
-        mhalf = keep.tile([P128, 1], F32, name="mhalf")
-        mone = keep.tile([P128, 1], F32, name="mone")
-        bcp = keep.tile([P128, 1024], BF16, name="bcp")
-        ident = keep.tile([P128, P128], F32, name="ident")
-        nc.vector.memset(bcs[:], 0.0)
-        nc.vector.memset(mone[:], -1.0)
-        nc.vector.memset(ones[:], 1.0)
-        nc.vector.memset(mhalf[:], -0.5)
-        nc.vector.memset(bcp[:], 0.0)
-        make_identity(nc, ident[:])
+        def small(name, n=1):
+            return keep.tile([P128, n], F32, name=name)
 
+        scb = keep.tile([P128, 64], BF16, name="scb")
         for col, src in enumerate((sine_w, cosine_w, w, p)):
-            nc.scalar.dma_start(
-                out=bcs[0:1, 16 * col : 16 * col + 1], in_=src.rearrange("(a b) -> a b", a=1)
-            )
-        nc.scalar.dma_start(out=bcp[0:1, :], in_=P.rearrange("(a n) -> a n", a=1))
+            nc.scalar.dma_start(out=scb[:, 16 * col : 16 * col + 1], in_=src.partition_broadcast(P128))
+        one = small("one")
+        prow = keep.tile([P128, P128], BF16, name="prow")
+        ident = keep.tile([P128, P128], F32, name="ident")
+        identb = keep.tile([P128, 8], BF16, name="identb")
+        nc.vector.memset(one[:], 1.0)
+        nc.vector.memset(prow[:], 0.0)
+        make_identity(nc, ident[:])
+        nc.scalar.dma_start(out=prow[0:8, :], in_=P.rearrange("(t q) -> t q", q=P128))
 
         x_sb = [keep.tile([P128, 1024], BF16, name="x_sb%d" % i) for i in range(NT)]
         w_raw = [[keep.tile([P128, 4, 512], BF16, name="w_raw%d%d" % (g, h)) for h in range(2)] for g in range(2)]
@@ -62,69 +62,28 @@ def tile_time2vec_kernel(tc, x, W, P, w, p, sine_w, cosine_w, out):
             )
 
         load_w(0, 0)
-        load_x(0)
         load_w(1, 0)
-        load_x(1)
+        for i in range(4):
+            load_x(i)
         load_w(0, 1)
-        load_x(2)
         load_w(1, 1)
-        for i in range(3, NT):
+        for i in range(4, NT):
             load_x(i)
 
-        ks = keep.tile([P128, 16], F32, name="ks")
-        kg = keep.tile([P128, 16], F32, name="kg")
-        sc = keep.tile([P128, 4], F32, name="sc")
+        junk = small("junk")
+        nc.scalar.activation(out=junk[:], in_=one[:], func=ACT.Abs_reciprocal_sqrt)
 
-        def kcol(t, j, n=1):
-            return t[:, j : j + n]
-
-        nc.scalar.activation(out=kcol(ks, 15), in_=mone[:], func=ACT.Sin)
-
-        ps_sc = psum.tile([P128, 64], F32, name="ps_sc", tag="xt", bufs=2)
-        nc.tensor.matmul(out=ps_sc[:], lhsT=ones[:], rhs=bcs[:], start=True, stop=True)
-        nc.vector.tensor_copy(out=sc[:], in_=ps_sc[:, 0:64:16])
-
-        swcw = sc[:, 0:2]
-        ab = kcol(ks, 0, 2)
-        nc.scalar.activation(out=ab, in_=swcw, func=ACT.Abs)
-        mx, rm, scn, t2, q, r, cs = kcol(kg, 0), kcol(kg, 1), kcol(kg, 2, 2), kcol(kg, 4, 2), kcol(kg, 6), kcol(kg, 7), kcol(kg, 8, 2)
-        c0, s0 = kcol(kg, 8), kcol(kg, 9)
-        gsg, hp, mm, phi0, g2, nc0 = kcol(kg, 10), kcol(kg, 11), kcol(kg, 12), kcol(kg, 13), kcol(kg, 14), kcol(kg, 15)
-        nc.gpsimd.tensor_scalar(out=mx, in0=kcol(ks, 0), scalar1=kcol(ks, 1), scalar2=1e-30, op0=ALU.max, op1=ALU.max)
-        nc.gpsimd.tensor_tensor(out=rm, in0=mx, in1=mone[:], op=ALU.pow)
-        nc.gpsimd.tensor_scalar(out=scn, in0=swcw, scalar1=rm, scalar2=None, op0=ALU.mult)
-        nc.gpsimd.tensor_tensor(out=t2, in0=scn, in1=scn, op=ALU.mult)
-        nc.gpsimd.tensor_scalar(out=q, in0=kcol(kg, 4), scalar1=kcol(kg, 5), scalar2=1e-30, op0=ALU.add, op1=ALU.max)
-        nc.gpsimd.tensor_tensor(out=r, in0=q, in1=mhalf[:], op=ALU.pow)
-        nc.gpsimd.tensor_scalar(out=cs, in0=scn, scalar1=r, scalar2=None, op0=ALU.mult)
-        nc.gpsimd.tensor_scalar(out=gsg, in0=s0, scalar1=0.0, scalar2=0.5, op0=ALU.is_ge, op1=ALU.subtract)
-        nc.gpsimd.tensor_scalar(out=hp, in0=c0, scalar1=-math.pi, scalar2=math.pi, op0=ALU.mult, op1=ALU.add)
-        nc.gpsimd.tensor_scalar(out=mm, in0=c0, scalar1=s0, scalar2=GUESS, op0=ALU.mult, op1=ALU.mult)
-        nc.gpsimd.tensor_scalar(out=phi0, in0=gsg, scalar1=hp, scalar2=mm, op0=ALU.mult, op1=ALU.add)
-        nc.gpsimd.tensor_scalar(out=g2, in0=gsg, scalar1=-2.0, scalar2=0.0, op0=ALU.mult, op1=ALU.add)
-        nc.gpsimd.tensor_scalar(out=nc0, in0=c0, scalar1=-1.0, scalar2=0.0, op0=ALU.mult, op1=ALU.add)
-
-        amp = kcol(ks, 14)
-        phi = kcol(ks, 13)
-
-        def phase_on_scalar():
-            cur = phi0
-            for it in range(2):
-                sn, cn, u = kcol(ks, 2 + 4 * it), kcol(ks, 3 + 4 * it), kcol(ks, 4 + 4 * it)
-                nxt = phi if it == 1 else kcol(ks, 5)
-                nc.scalar.activation(out=sn, in_=cur, func=ACT.Sin)
-                nc.scalar.activation(out=cn, in_=cur, func=ACT.Sin, bias=0.5 * math.pi, scale=g2)
-                nc.scalar.activation(out=u, in_=cn, func=ACT.Identity, bias=cur, scale=s0)
-                nc.scalar.activation(out=nxt, in_=sn, func=ACT.Identity, bias=u, scale=nc0)
-                cur = nxt
-            t = kcol(ks, 10)
-            nc.scalar.activation(out=t, in_=kcol(ks, 6), func=ACT.Copy, scale=sc[:, 1:2])
-            nc.scalar.activation(out=amp, in_=kcol(ks, 7), func=ACT.Identity, bias=t, scale=sc[:, 0:1])
+        nc.vector.tensor_copy(out=identb[:], in_=ident[:, 0:8])
+        ps_p = psum.tile([P128, 8], F32, name="ps_p", tag="tp", bufs=4)
+        nc.tensor.matmul(out=ps_p[:], lhsT=prow[:], rhs=identb[:], start=True, stop=True)
+        pt = small("pt", 8)
+        nc.vector.tensor_copy(out=pt[:], in_=ps_p[:])
 
         wg = [[keep.tile([P128, 2048], BF16, name="wg%d%d" % (g, h), align_bytes=64) for h in range(2)] for g in range(2)]
         wq = [[keep.tile([P128, 512], U32, name="wq%d%d" % (g, h), align_bytes=64) for h in range(2)] for g in range(2)]
         ws = [[keep.tile([P128, 512], U8, name="ws%d%d" % (g, h), align_bytes=64) for h in range(2)] for g in range(2)]
-        pb = keep.tile([P128, 1024], F32, name="pb")
+        xq = [[keep.tile([P128, 512], U32, name="xq%d%d" % (g, h), align_bytes=64) for h in range(2)] for g in range(2)]
+        xs = [[keep.tile([P128, 512], U8, name="xs%d%d" % (g, h), align_bytes=64) for h in range(2)] for g in range(2)]
         st = {}
 
         def interleave_w(g, h):
@@ -137,7 +96,7 @@ def tile_time2vec_kernel(tc, x, W, P, w, p, sine_w, cosine_w, out):
             nc.vector.quantize_mx(out=wq[g][h][:].bitcast(E5X4), scales=ws[g][h][:], in_=wg[g][h][:])
 
         def transpose_x(i):
-            xt = psum.tile([P128, 512], F32, name="xt", tag="xt", bufs=2)
+            xt = psum.tile([P128, 512], F32, name="xt", tag="tp", bufs=4)
             st["xt", i] = xt
             words = x_sb[i][:].bitcast(F32)
             for g in range(2):
@@ -146,7 +105,7 @@ def tile_time2vec_kernel(tc, x, W, P, w, p, sine_w, cosine_w, out):
                     nc.tensor.transpose(xt[:, 128 * c : 128 * (c + 1)], words[:, 256 * g + u : 256 * (g + 1) : 2], ident[:])
 
         def copy_x(i):
-            xg = work.tile([P128, 1024], BF16, name="xg", tag="xg", bufs=3, align_bytes=64)
+            xg = work.tile([P128, 1024], BF16, name="xg", tag="xg", bufs=4, align_bytes=64)
             st["xg", i] = xg
             nc.scalar.copy(
                 out=xg[:].bitcast(F32).rearrange("p (g r u) -> p g r u", g=2, u=2),
@@ -154,124 +113,205 @@ def tile_time2vec_kernel(tc, x, W, P, w, p, sine_w, cosine_w, out):
             )
 
         def quantize_x(i):
-            xq = work.tile([P128, 256], U32, name="xq", tag="xq", bufs=3, align_bytes=64)
-            xs = work.tile([P128, 256], U8, name="xs", tag="xs", bufs=3, align_bytes=64)
-            st["xq", i] = xq
-            st["xs", i] = xs
-            nc.vector.quantize_mx(out=xq[:].bitcast(E5X4), scales=xs[:], in_=st["xg", i][:])
+            hb, iq = i // 4, i % 4
+            for g in range(2):
+                nc.vector.quantize_mx(
+                    out=xq[g][hb][:, 128 * iq : 128 * (iq + 1)].bitcast(E5X4),
+                    scales=xs[g][hb][:, 128 * iq : 128 * (iq + 1)],
+                    in_=st["xg", i][:, 512 * g : 512 * (g + 1)],
+                )
 
-        def matmuls(i):
-            for h in range(2):
-                acc = psum.tile([P128, 512], F32, name="acc", tag="acc", bufs=4)
-                st["acc", i, h] = acc
-                for g in range(2):
-                    nc.tensor.matmul_mx(
-                        out=acc[:],
-                        lhsT=st["xq", i][:, 128 * g : 128 * (g + 1)].bitcast(E5X4),
-                        lhsT_scale=st["xs", i][:, 128 * g : 128 * (g + 1)],
-                        rhs=wq[g][h][:].bitcast(E5X4),
-                        rhs_scale=ws[g][h][:],
-                        start=(g == 0),
-                        stop=(g == 1),
-                    )
+        def matmuls(u):
+            hb, nh = GROUPS[u // 4]
+            tq = u % 4
+            acc = psum.tile([P128, 512], F32, name="acc", tag="acc", bufs=4)
+            st["acc", u] = acc
+            for g in range(2):
+                nc.tensor.matmul_mx(
+                    out=acc[:],
+                    lhsT=wq[g][nh][:, 128 * tq : 128 * (tq + 1)].bitcast(E5X4),
+                    lhsT_scale=ws[g][nh][:, 128 * tq : 128 * (tq + 1)],
+                    rhs=xq[g][hb][:].bitcast(E5X4),
+                    rhs_scale=xs[g][hb][:],
+                    start=(g == 0),
+                    stop=(g == 1),
+                )
 
-        def turns(i, h):
-            if h == 0:
-                st["v", i] = work.tile([P128, 1024], F32, name="v", tag="v", bufs=3)
-            nc.vector.scalar_tensor_tensor(
-                out=st["v", i][:, 512 * h : 512 * (h + 1)],
-                in0=st["acc", i, h][:],
-                scalar=INV_2PI,
-                in1=pb[:, 512 * h : 512 * (h + 1)],
-                op0=ALU.mult,
-                op1=ALU.add,
+        sc = small("sc", 4)
+        ab, c1s1, t2, cs = small("ab", 2), small("c1s1", 2), small("t2", 2), small("cs", 2)
+        dd, rs, rd, qq, rr = small("dd"), small("rs"), small("rd"), small("qq"), small("rr")
+        sg, hh, m0, nsg, nc0, hs = small("sg"), small("hh"), small("m0"), small("nsg"), small("nc0"), small("hs")
+        ph = [small("ph%d" % k) for k in range(3)]
+        sn = [small("sn%d" % k) for k in range(2)]
+        cn = [small("cn%d" % k) for k in range(2)]
+        uu = [small("uu%d" % k) for k in range(2)]
+        ta, amp = small("ta"), small("amp")
+        brad, bturn = small("brad", 8), small("bturn", 8)
+        c0, s0 = cs[:, 0:1], cs[:, 1:2]
+        act = nc.scalar.activation
+
+        def chain_a():
+            nc.scalar.copy(out=sc[:], in_=scb[:, 0:64:16])
+            act(out=ab[:], in_=sc[:, 0:2], func=ACT.Abs, bias=TINY, scale=0.5)
+            act(out=dd[:], in_=ab[:, 0:1], func=ACT.Identity, bias=ab[:, 1:2])
+            act(out=rs[:], in_=dd[:], func=ACT.Abs_reciprocal_sqrt)
+            act(out=rd[:], in_=rs[:], func=ACT.Square)
+            act(out=c1s1[:], in_=sc[:, 0:2], func=ACT.Copy, scale=rd[:])
+            act(out=t2[:], in_=c1s1[:], func=ACT.Square)
+            act(out=qq[:], in_=t2[:, 0:1], func=ACT.Identity, bias=t2[:, 1:2])
+            act(out=rr[:], in_=qq[:], func=ACT.Abs_reciprocal_sqrt, bias=TINY)
+            act(out=cs[:], in_=c1s1[:], func=ACT.Copy, scale=rr[:])
+            act(out=sg[:], in_=s0, func=ACT.Sign, bias=TINY)
+            act(out=hh[:], in_=c0, func=ACT.Identity, bias=0.5 * math.pi, scale=-0.5 * math.pi)
+            act(out=m0[:], in_=c0, func=ACT.Copy, scale=s0)
+            act(out=nc0[:], in_=c0, func=ACT.Copy, scale=-1.0)
+            act(out=nsg[:], in_=sg[:], func=ACT.Copy, scale=-1.0)
+            act(out=hs[:], in_=hh[:], func=ACT.Copy, scale=sg[:])
+
+        def chain_guess():
+            act(out=ph[0][:], in_=m0[:], func=ACT.Identity, bias=hs[:], scale=GUESS)
+
+        def chain_sincos(k):
+            act(out=sn[k][:], in_=ph[k][:], func=ACT.Sin)
+            act(out=cn[k][:], in_=ph[k][:], func=ACT.Sin, bias=0.5 * math.pi, scale=nsg[:])
+
+        def chain_u(k):
+            act(out=uu[k][:], in_=cn[k][:], func=ACT.Identity, bias=ph[k][:], scale=s0)
+
+        def chain_next(k):
+            act(out=ph[k + 1][:], in_=sn[k][:], func=ACT.Identity, bias=uu[k][:], scale=nc0[:])
+
+        def cols(k):
+            u, b0, b1 = PIECES[k]
+            return u, slice(128 * b0, 128 * b1), 128 * (b1 - b0)
+
+        def whole_turns(k):
+            u, cc, width = cols(k)
+            t = 4 * GROUPS[u // 4][1] + u % 4
+            n = work.tile([P128, width], I32, name="n", tag="n", bufs=3)
+            st["n", k] = n
+            nc.vector.tensor_scalar(
+                out=n[:], in0=st["acc", u][:, cc], scalar1=INV_2PI, scalar2=bturn[:, t : t + 1], op0=ALU.mult, op1=ALU.add
             )
 
-        def whole_turns(i):
-            n = work.tile([P128, 1024], I32, name="n", tag="n", bufs=2)
-            st["n", i] = n
-            nc.vector.tensor_copy(out=n[:], in_=st["v", i][:])
+        def fraction(k):
+            u, cc, width = cols(k)
+            f = work.tile([P128, width], F32, name="f", tag="f", bufs=3)
+            st["f", k] = f
+            nc.vector.scalar_tensor_tensor(
+                out=f[:], in0=st["acc", u][:, cc], scalar=INV_2PI, in1=st["n", k][:], op0=ALU.mult, op1=ALU.subtract
+            )
 
-        def fraction(i):
-            f = work.tile([P128, 1024], F32, name="f", tag="f", bufs=2)
-            st["f", i] = f
-            nc.vector.tensor_tensor(out=f[:], in0=st["v", i][:], in1=st["n", i][:], op=ALU.subtract)
+        def sine(k):
+            u, cc, width = cols(k)
+            t = 4 * GROUPS[u // 4][1] + u % 4
+            s = work.tile([P128, width], F32, name="s", tag="s", bufs=4)
+            st["s", k] = s
+            act(out=s[:], in_=st["f", k][:], func=ACT.Sin, bias=brad[:, t : t + 1], scale=TWO_PI)
 
-        def sine(i):
-            s = work.tile([P128, 1024], F32, name="s", tag="s", bufs=2)
-            st["s", i] = s
-            nc.scalar.activation(out=s[:], in_=st["f", i][:], func=ACT.Sin, scale=TWO_PI)
+        def transpose_back(k):
+            u, cc, width = cols(k)
+            tp = psum.tile([P128, width], F32, name="tp", tag="tp", bufs=4)
+            st["tp", k] = tp
+            for b in range(width // 128):
+                nc.tensor.transpose(tp[:, 128 * b : 128 * (b + 1)], st["s", k][:, 128 * b : 128 * (b + 1)], ident[:])
 
-        def scale_store(i):
-            o = work.tile([P128, 1024], F32, name="o", tag="o", bufs=3)
-            nc.scalar.activation(out=o[:], in_=st["s", i][:], func=ACT.Copy, scale=amp)
-            nc.sync.dma_start(out=out[128 * i : 128 * (i + 1), 1024:2048], in_=o[:])
+        run_of = {}
+        first = 0
+        for length in RUNS:
+            for u in range(first, first + length):
+                run_of[u] = (first, length)
+            first += length
+
+        def scale_store(k):
+            u, b0, b1 = PIECES[k]
+            first_u, length = run_of[u]
+            nb = b1 - b0
+            if ("o", first_u, b0) not in st:
+                st["o", first_u, b0] = keep.tile([P128, nb, 128 * length], F32, name="o%d_%d" % (first_u, b0))
+            o = st["o", first_u, b0]
+            c = 128 * (u - first_u)
+            act(
+                out=o[:, :, c : c + 128],
+                in_=st["tp", k][:].rearrange("p (i n) -> p i n", n=128),
+                func=ACT.Copy,
+                scale=amp[:],
+            )
+            if u == first_u + length - 1:
+                hb, nh = GROUPS[u // 4]
+                r0 = 512 * hb + 128 * b0
+                c0d = 1024 + 512 * nh + 128 * (first_u % 4)
+                nc.sync.dma_start(
+                    out=out[r0 : r0 + 128 * nb, c0d : c0d + 128 * length].rearrange("(i q) n -> q i n", q=P128),
+                    in_=o[:],
+                )
+
+        wpl = small("wpl", 2)
 
         def linear(i):
-            lin = work.tile([P128, 1024], F32, name="lin", tag="lin", bufs=3)
-            nc.scalar.activation(out=lin[:], in_=x_sb[i][:], func=ACT.Identity, bias=sc[:, 3:4], scale=sc[:, 2:3])
+            lin = work.tile([P128, 1024], F32, name="lin", tag="lin", bufs=4)
+            nc.gpsimd.tensor_scalar(
+                out=lin[:], in0=x_sb[i][:], scalar1=wpl[:, 0:1], scalar2=wpl[:, 1:2], op0=ALU.mult, op1=ALU.add
+            )
             nc.sync.dma_start(out=out[128 * i : 128 * (i + 1), 0:1024], in_=lin[:])
 
-        def bias_rows():
-            for h in range(2):
-                psp = psum.tile([P128, 512], F32, name="psp", tag="acc", bufs=4)
-                st["psp", h] = psp
-                nc.tensor.matmul(out=psp[:], lhsT=ones[:], rhs=bcp[:, 512 * h : 512 * (h + 1)], start=True, stop=True)
-
-        def bias_turns(h):
-            nc.vector.tensor_scalar(
-                out=pb[:, 512 * h : 512 * (h + 1)], in0=st["psp", h][:], scalar1=phi, scalar2=INV_2PI, op0=ALU.add, op1=ALU.mult
-            )
-
         interleave_w(0, 0)
-        transpose_x(0)
-        copy_x(0)
-        linear(0)
         interleave_w(1, 0)
-        transpose_x(1)
-        copy_x(1)
-        linear(1)
         quantize_w(0, 0)
         quantize_w(1, 0)
+        for i in range(4):
+            transpose_x(i)
+        chain_a()
+        copy_x(0)
         quantize_x(0)
-        phase_on_scalar()
-        bias_rows()
-        interleave_w(0, 1)
-        transpose_x(2)
-        copy_x(2)
-        linear(2)
-        interleave_w(1, 1)
+        transpose_x(4)
+        chain_guess()
+        chain_sincos(0)
+        copy_x(1)
         quantize_x(1)
-        transpose_x(3)
+        transpose_x(5)
+        interleave_w(0, 1)
+        chain_u(0)
+        copy_x(2)
+        quantize_x(2)
+        transpose_x(6)
+        chain_next(0)
         copy_x(3)
-        linear(3)
+        quantize_x(3)
+        transpose_x(7)
+        for u in range(4):
+            matmuls(u)
+        interleave_w(1, 1)
+        chain_sincos(1)
+        copy_x(4)
+        chain_u(1)
+        act(out=ta[:], in_=sn[1][:], func=ACT.Copy, scale=sc[:, 1:2])
+        copy_x(5)
+        chain_next(1)
+        act(out=amp[:], in_=cn[1][:], func=ACT.Identity, bias=ta[:], scale=sc[:, 0:1])
+        copy_x(6)
+        act(out=brad[:], in_=pt[:], func=ACT.Identity, bias=ph[2][:])
+        copy_x(7)
+        act(out=bturn[:], in_=brad[:], func=ACT.Copy, scale=INV_2PI)
         quantize_w(0, 1)
         quantize_w(1, 1)
-        bias_turns(0)
-        bias_turns(1)
-        quantize_x(2)
-        matmuls(0)
-        matmuls(1)
+        for i in range(4, NT):
+            quantize_x(i)
+        nc.vector.tensor_copy(out=wpl[:], in_=sc[:, 2:4])
 
-        for i in range(NT + 1):
-            if i < NT:
-                turns(i, 0)
-                turns(i, 1)
-            if i >= 1:
-                fraction(i - 1)
-            if i < NT:
-                whole_turns(i)
-            if i + 3 < NT:
-                quantize_x(i + 3)
-            if i + 2 < NT:
-                matmuls(i + 2)
-            if i + 4 < NT:
-                transpose_x(i + 4)
-            if i >= 1:
-                sine(i - 1)
-            if i + 4 < NT:
-                copy_x(i + 4)
-            if i >= 1:
-                scale_store(i - 1)
-            if i + 4 < NT:
-                linear(i + 4)
+        npieces = len(PIECES)
+        for s in range(npieces + 3):
+            if s < npieces:
+                whole_turns(s)
+            if 1 <= s <= npieces:
+                fraction(s - 1)
+            if 3 <= s:
+                transpose_back(s - 3)
+            if 4 <= s + 3 <= 15:
+                matmuls(s + 3)
+            if 1 <= s <= npieces:
+                sine(s - 1)
+            if 3 <= s:
+                scale_store(s - 3)
+            if s < NT:
+                linear(s)

@@ -22,7 +22,9 @@ INV_2PI = 1.0 / (2.0 * math.pi)
 GUESS = 0.68
 TINY = 1e-30
 GROUPS = ((0, 0), (1, 0), (0, 1), (1, 1))
-RUNS = (4, 4, 4, 2, 1, 1)
+RUNS = (4, 4, 2, 2, 2, 1, 1)
+ON_VECTOR = (13, 15, 16)
+X_ON_VECTOR = (3, 5, 7)
 PIECES = [(u, 0, 4) for u in range(15)] + [(15, 0, 2), (15, 2, 4)]
 
 
@@ -39,7 +41,7 @@ def tile_time2vec_kernel(tc, x, W, P, w, p, sine_w, cosine_w, out):
 
         scb = keep.tile([P128, 64], BF16, name="scb")
         for col, src in enumerate((sine_w, cosine_w, w, p)):
-            nc.scalar.dma_start(out=scb[:, 16 * col : 16 * col + 1], in_=src.partition_broadcast(P128))
+            nc.sync.dma_start(out=scb[:, 16 * col : 16 * col + 1], in_=src.partition_broadcast(P128))
         one = small("one")
         prow = keep.tile([P128, P128], BF16, name="prow")
         ident = keep.tile([P128, P128], F32, name="ident")
@@ -47,7 +49,7 @@ def tile_time2vec_kernel(tc, x, W, P, w, p, sine_w, cosine_w, out):
         nc.vector.memset(one[:], 1.0)
         nc.vector.memset(prow[:], 0.0)
         make_identity(nc, ident[:])
-        nc.scalar.dma_start(out=prow[0:8, :], in_=P.rearrange("(t q) -> t q", q=P128))
+        nc.sync.dma_start(out=prow[0:8, :], in_=P.rearrange("(t q) -> t q", q=P128))
 
         x_sb = [keep.tile([P128, 1024], BF16, name="x_sb%d" % i) for i in range(NT)]
         w_raw = [[keep.tile([P128, 4, 512], BF16, name="w_raw%d%d" % (g, h)) for h in range(2)] for g in range(2)]
@@ -63,21 +65,17 @@ def tile_time2vec_kernel(tc, x, W, P, w, p, sine_w, cosine_w, out):
 
         load_w(0, 0)
         load_w(1, 0)
-        for i in range(4):
-            load_x(i)
         load_w(0, 1)
         load_w(1, 1)
-        for i in range(4, NT):
+        for i in range(NT):
             load_x(i)
 
         junk = small("junk")
         nc.scalar.activation(out=junk[:], in_=one[:], func=ACT.Abs_reciprocal_sqrt)
 
         nc.vector.tensor_copy(out=identb[:], in_=ident[:, 0:8])
-        ps_p = psum.tile([P128, 8], F32, name="ps_p", tag="tp", bufs=4)
+        ps_p = psum.tile([P128, 8], F32, name="ps_p", tag="acc", bufs=4)
         nc.tensor.matmul(out=ps_p[:], lhsT=prow[:], rhs=identb[:], start=True, stop=True)
-        pt = small("pt", 8)
-        nc.vector.tensor_copy(out=pt[:], in_=ps_p[:])
 
         wg = [[keep.tile([P128, 2048], BF16, name="wg%d%d" % (g, h), align_bytes=64) for h in range(2)] for g in range(2)]
         wq = [[keep.tile([P128, 512], U32, name="wq%d%d" % (g, h), align_bytes=64) for h in range(2)] for g in range(2)]
@@ -88,8 +86,8 @@ def tile_time2vec_kernel(tc, x, W, P, w, p, sine_w, cosine_w, out):
 
         def interleave_w(g, h):
             nc.vector.tensor_copy(
-                out=wg[g][h][:].rearrange("p (n j) -> p n j", j=4),
-                in_=w_raw[g][h][:].rearrange("p j n -> p n j"),
+                out=wg[g][h][:].rearrange("p (c i j) -> p c j i", i=4, j=4),
+                in_=w_raw[g][h][:].rearrange("p j (c i) -> p c j i", i=4),
             )
 
         def quantize_w(g, h):
@@ -105,9 +103,10 @@ def tile_time2vec_kernel(tc, x, W, P, w, p, sine_w, cosine_w, out):
                     nc.tensor.transpose(xt[:, 128 * c : 128 * (c + 1)], words[:, 256 * g + u : 256 * (g + 1) : 2], ident[:])
 
         def copy_x(i):
-            xg = work.tile([P128, 1024], BF16, name="xg", tag="xg", bufs=4, align_bytes=64)
+            xg = work.tile([P128, 1024], BF16, name="xg", tag="xg", bufs=8, align_bytes=64)
             st["xg", i] = xg
-            nc.scalar.copy(
+            copy = nc.vector.tensor_copy if i in X_ON_VECTOR else nc.scalar.copy
+            copy(
                 out=xg[:].bitcast(F32).rearrange("p (g r u) -> p g r u", g=2, u=2),
                 in_=st["xt", i][:].rearrange("p (g u r) -> p g r u", g=2, u=2),
             )
@@ -139,47 +138,44 @@ def tile_time2vec_kernel(tc, x, W, P, w, p, sine_w, cosine_w, out):
 
         sc = small("sc", 4)
         ab, c1s1, t2, cs = small("ab", 2), small("c1s1", 2), small("t2", 2), small("cs", 2)
-        dd, rs, rd, qq, rr = small("dd"), small("rs"), small("rd"), small("qq"), small("rr")
+        dd, rs, rd, rr = small("dd"), small("rs"), small("rd"), small("rr")
         sg, hh, m0, nsg, nc0, hs = small("sg"), small("hh"), small("m0"), small("nsg"), small("nc0"), small("hs")
         ph = [small("ph%d" % k) for k in range(3)]
         sn = [small("sn%d" % k) for k in range(2)]
         cn = [small("cn%d" % k) for k in range(2)]
         uu = [small("uu%d" % k) for k in range(2)]
         ta, amp = small("ta"), small("amp")
-        brad, bturn = small("brad", 8), small("bturn", 8)
+        brad = small("brad", 8)
         c0, s0 = cs[:, 0:1], cs[:, 1:2]
+        swcw = scb[:, 0:32:16]
         act = nc.scalar.activation
 
-        def chain_a():
-            nc.scalar.copy(out=sc[:], in_=scb[:, 0:64:16])
-            act(out=ab[:], in_=sc[:, 0:2], func=ACT.Abs, bias=TINY, scale=0.5)
+        def chain():
+            act(out=ab[:], in_=swcw, func=ACT.Abs, bias=TINY, scale=0.5)
             act(out=dd[:], in_=ab[:, 0:1], func=ACT.Identity, bias=ab[:, 1:2])
             act(out=rs[:], in_=dd[:], func=ACT.Abs_reciprocal_sqrt)
             act(out=rd[:], in_=rs[:], func=ACT.Square)
-            act(out=c1s1[:], in_=sc[:, 0:2], func=ACT.Copy, scale=rd[:])
-            act(out=t2[:], in_=c1s1[:], func=ACT.Square)
-            act(out=qq[:], in_=t2[:, 0:1], func=ACT.Identity, bias=t2[:, 1:2])
-            act(out=rr[:], in_=qq[:], func=ACT.Abs_reciprocal_sqrt, bias=TINY)
+            act(out=t2[:], in_=swcw, func=ACT.Square, bias=1e-18, scale=rd[:])
+            act(out=c1s1[:], in_=swcw, func=ACT.Copy, scale=rd[:])
+            act(out=rr[:], in_=t2[:, 0:1], func=ACT.Abs_reciprocal_sqrt, bias=t2[:, 1:2])
+            act(out=junk[:], in_=one[:], func=ACT.Sin)
             act(out=cs[:], in_=c1s1[:], func=ACT.Copy, scale=rr[:])
             act(out=sg[:], in_=s0, func=ACT.Sign, bias=TINY)
             act(out=hh[:], in_=c0, func=ACT.Identity, bias=0.5 * math.pi, scale=-0.5 * math.pi)
             act(out=m0[:], in_=c0, func=ACT.Copy, scale=s0)
             act(out=nc0[:], in_=c0, func=ACT.Copy, scale=-1.0)
-            act(out=nsg[:], in_=sg[:], func=ACT.Copy, scale=-1.0)
             act(out=hs[:], in_=hh[:], func=ACT.Copy, scale=sg[:])
-
-        def chain_guess():
+            act(out=nsg[:], in_=sg[:], func=ACT.Copy, scale=-1.0)
             act(out=ph[0][:], in_=m0[:], func=ACT.Identity, bias=hs[:], scale=GUESS)
-
-        def chain_sincos(k):
-            act(out=sn[k][:], in_=ph[k][:], func=ACT.Sin)
-            act(out=cn[k][:], in_=ph[k][:], func=ACT.Sin, bias=0.5 * math.pi, scale=nsg[:])
-
-        def chain_u(k):
-            act(out=uu[k][:], in_=cn[k][:], func=ACT.Identity, bias=ph[k][:], scale=s0)
-
-        def chain_next(k):
-            act(out=ph[k + 1][:], in_=sn[k][:], func=ACT.Identity, bias=uu[k][:], scale=nc0[:])
+            for k in range(2):
+                act(out=sn[k][:], in_=ph[k][:], func=ACT.Sin)
+                act(out=cn[k][:], in_=ph[k][:], func=ACT.Sin, bias=0.5 * math.pi, scale=nsg[:])
+                act(out=uu[k][:], in_=cn[k][:], func=ACT.Identity, bias=ph[k][:], scale=s0)
+                if k == 1:
+                    act(out=ta[:], in_=sn[1][:], func=ACT.Copy, scale=sc[:, 1:2])
+                act(out=ph[k + 1][:], in_=sn[k][:], func=ACT.Identity, bias=uu[k][:], scale=nc0[:])
+            act(out=brad[:], in_=ps_p[:], func=ACT.Identity, bias=ph[2][:])
+            act(out=amp[:], in_=cn[1][:], func=ACT.Identity, bias=ta[:], scale=sc[:, 0:1])
 
         def cols(k):
             u, b0, b1 = PIECES[k]
@@ -191,7 +187,7 @@ def tile_time2vec_kernel(tc, x, W, P, w, p, sine_w, cosine_w, out):
             n = work.tile([P128, width], I32, name="n", tag="n", bufs=3)
             st["n", k] = n
             nc.vector.tensor_scalar(
-                out=n[:], in0=st["acc", u][:, cc], scalar1=INV_2PI, scalar2=bturn[:, t : t + 1], op0=ALU.mult, op1=ALU.add
+                out=n[:], in0=st["acc", u][:, cc], scalar1=brad[:, t : t + 1], scalar2=INV_2PI, op0=ALU.add, op1=ALU.mult
             )
 
         def fraction(k):
@@ -205,7 +201,7 @@ def tile_time2vec_kernel(tc, x, W, P, w, p, sine_w, cosine_w, out):
         def sine(k):
             u, cc, width = cols(k)
             t = 4 * GROUPS[u // 4][1] + u % 4
-            s = work.tile([P128, width], F32, name="s", tag="s", bufs=4)
+            s = work.tile([P128, width], F32, name="s", tag="s", bufs=5)
             st["s", k] = s
             act(out=s[:], in_=st["f", k][:], func=ACT.Sin, bias=brad[:, t : t + 1], scale=TWO_PI)
 
@@ -231,12 +227,11 @@ def tile_time2vec_kernel(tc, x, W, P, w, p, sine_w, cosine_w, out):
                 st["o", first_u, b0] = keep.tile([P128, nb, 128 * length], F32, name="o%d_%d" % (first_u, b0))
             o = st["o", first_u, b0]
             c = 128 * (u - first_u)
-            act(
-                out=o[:, :, c : c + 128],
-                in_=st["tp", k][:].rearrange("p (i n) -> p i n", n=128),
-                func=ACT.Copy,
-                scale=amp[:],
-            )
+            banked = st["tp", k][:].rearrange("p (i n) -> p i n", n=128)
+            if k in ON_VECTOR:
+                nc.vector.tensor_scalar(out=o[:, :, c : c + 128], in0=banked, scalar1=amp[:], scalar2=None, op0=ALU.mult)
+            else:
+                act(out=o[:, :, c : c + 128], in_=banked, func=ACT.Copy, scale=amp[:])
             if u == first_u + length - 1:
                 hb, nh = GROUPS[u // 4]
                 r0 = 512 * hb + 128 * b0
@@ -256,62 +251,48 @@ def tile_time2vec_kernel(tc, x, W, P, w, p, sine_w, cosine_w, out):
             nc.sync.dma_start(out=out[128 * i : 128 * (i + 1), 0:1024], in_=lin[:])
 
         interleave_w(0, 0)
+        nc.vector.tensor_copy(out=sc[:], in_=scb[:, 0:64:16])
         interleave_w(1, 0)
         quantize_w(0, 0)
-        quantize_w(1, 0)
-        for i in range(4):
-            transpose_x(i)
-        chain_a()
-        copy_x(0)
-        quantize_x(0)
-        transpose_x(4)
-        chain_guess()
-        chain_sincos(0)
-        copy_x(1)
-        quantize_x(1)
-        transpose_x(5)
         interleave_w(0, 1)
-        chain_u(0)
-        copy_x(2)
-        quantize_x(2)
-        transpose_x(6)
-        chain_next(0)
-        copy_x(3)
-        quantize_x(3)
-        transpose_x(7)
-        for u in range(4):
-            matmuls(u)
+        quantize_w(1, 0)
         interleave_w(1, 1)
-        chain_sincos(1)
-        copy_x(4)
-        chain_u(1)
-        act(out=ta[:], in_=sn[1][:], func=ACT.Copy, scale=sc[:, 1:2])
-        copy_x(5)
-        chain_next(1)
-        act(out=amp[:], in_=cn[1][:], func=ACT.Identity, bias=ta[:], scale=sc[:, 0:1])
-        copy_x(6)
-        act(out=brad[:], in_=pt[:], func=ACT.Identity, bias=ph[2][:])
-        copy_x(7)
-        act(out=bturn[:], in_=brad[:], func=ACT.Copy, scale=INV_2PI)
         quantize_w(0, 1)
         quantize_w(1, 1)
-        for i in range(4, NT):
-            quantize_x(i)
+        chain()
+        for i in range(4):
+            transpose_x(i)
+        for i in range(NT):
+            copy_x(i)
+            if i + 4 < NT:
+                transpose_x(i + 4)
+            if i >= 1:
+                quantize_x(i - 1)
+        quantize_x(NT - 1)
+        for u in range(4):
+            matmuls(u)
         nc.vector.tensor_copy(out=wpl[:], in_=sc[:, 2:4])
 
         npieces = len(PIECES)
+        paired = 10
+        back_at, out_at, mx_at = {}, {}, {}
+        for k in range(npieces):
+            back_at.setdefault(2 * (k // 2) + 4 if k < paired else k + 3, []).append(k)
+            out_at.setdefault(k + 4 if k < paired else k + 3, []).append(k)
+        for u in range(4, 16):
+            mx_at.setdefault(2 * (u // 2) - 2, []).append(u)
         for s in range(npieces + 3):
             if s < npieces:
                 whole_turns(s)
             if 1 <= s <= npieces:
                 fraction(s - 1)
-            if 3 <= s:
-                transpose_back(s - 3)
-            if 4 <= s + 3 <= 15:
-                matmuls(s + 3)
+            for k in back_at.get(s, []):
+                transpose_back(k)
+            for u in mx_at.get(s, []):
+                matmuls(u)
             if 1 <= s <= npieces:
                 sine(s - 1)
-            if 3 <= s:
-                scale_store(s - 3)
+            for k in out_at.get(s, []):
+                scale_store(k)
             if s < NT:
                 linear(s)

@@ -22,9 +22,11 @@ INV_2PI = 1.0 / (2.0 * math.pi)
 GUESS = 0.68
 TINY = 1e-30
 GROUPS = ((0, 0), (1, 0), (0, 1), (1, 1))
-RUNS = (4, 4, 2, 2, 2, 1, 1)
+RUNS = (2, 2, 2, 2, 2, 2, 2, 1, 1)
 ON_VECTOR = (13, 15, 16)
-X_ON_VECTOR = (3, 5, 7)
+X_ON_VECTOR = (1, 3, 5, 7)
+EARLY_LINEAR = 2
+LATE_W_STEP = 7
 PIECES = [(u, 0, 4) for u in range(15)] + [(15, 0, 2), (15, 2, 4)]
 
 
@@ -65,10 +67,10 @@ def tile_time2vec_kernel(tc, x, W, P, w, p, sine_w, cosine_w, out):
 
         load_w(0, 0)
         load_w(1, 0)
-        load_w(0, 1)
-        load_w(1, 1)
         for i in range(NT):
             load_x(i)
+        load_w(0, 1)
+        load_w(1, 1)
 
         junk = small("junk")
         nc.scalar.activation(out=junk[:], in_=one[:], func=ACT.Abs_reciprocal_sqrt)
@@ -83,11 +85,22 @@ def tile_time2vec_kernel(tc, x, W, P, w, p, sine_w, cosine_w, out):
         xq = [[keep.tile([P128, 512], U32, name="xq%d%d" % (g, h), align_bytes=64) for h in range(2)] for g in range(2)]
         xs = [[keep.tile([P128, 512], U8, name="xs%d%d" % (g, h), align_bytes=64) for h in range(2)] for g in range(2)]
         st = {}
+        gate = small("gate")
 
         def interleave_w(g, h):
             nc.vector.tensor_copy(
                 out=wg[g][h][:].rearrange("p (c i j) -> p c j i", i=4, j=4),
                 in_=w_raw[g][h][:].rearrange("p j (c i) -> p c j i", i=4),
+            )
+
+        def interleave_w_gpsimd(g, h):
+            nc.gpsimd.tensor_scalar(
+                out=wg[g][h][:].rearrange("p (n j) -> p n j", j=4),
+                in0=w_raw[g][h][:].rearrange("p j n -> p n j"),
+                scalar1=gate[:],
+                scalar2=0.0,
+                op0=ALU.mult,
+                op1=ALU.add,
             )
 
         def quantize_w(g, h):
@@ -150,7 +163,7 @@ def tile_time2vec_kernel(tc, x, W, P, w, p, sine_w, cosine_w, out):
         swcw = scb[:, 0:32:16]
         act = nc.scalar.activation
 
-        def chain():
+        def chain_norm():
             act(out=ab[:], in_=swcw, func=ACT.Abs, bias=TINY, scale=0.5)
             act(out=dd[:], in_=ab[:, 0:1], func=ACT.Identity, bias=ab[:, 1:2])
             act(out=rs[:], in_=dd[:], func=ACT.Abs_reciprocal_sqrt)
@@ -160,6 +173,8 @@ def tile_time2vec_kernel(tc, x, W, P, w, p, sine_w, cosine_w, out):
             act(out=rr[:], in_=t2[:, 0:1], func=ACT.Abs_reciprocal_sqrt, bias=t2[:, 1:2])
             act(out=junk[:], in_=one[:], func=ACT.Sin)
             act(out=cs[:], in_=c1s1[:], func=ACT.Copy, scale=rr[:])
+
+        def chain_guess():
             act(out=sg[:], in_=s0, func=ACT.Sign, bias=TINY)
             act(out=hh[:], in_=c0, func=ACT.Identity, bias=0.5 * math.pi, scale=-0.5 * math.pi)
             act(out=m0[:], in_=c0, func=ACT.Copy, scale=s0)
@@ -167,13 +182,15 @@ def tile_time2vec_kernel(tc, x, W, P, w, p, sine_w, cosine_w, out):
             act(out=hs[:], in_=hh[:], func=ACT.Copy, scale=sg[:])
             act(out=nsg[:], in_=sg[:], func=ACT.Copy, scale=-1.0)
             act(out=ph[0][:], in_=m0[:], func=ACT.Identity, bias=hs[:], scale=GUESS)
-            for k in range(2):
-                act(out=sn[k][:], in_=ph[k][:], func=ACT.Sin)
-                act(out=cn[k][:], in_=ph[k][:], func=ACT.Sin, bias=0.5 * math.pi, scale=nsg[:])
-                act(out=uu[k][:], in_=cn[k][:], func=ACT.Identity, bias=ph[k][:], scale=s0)
-                if k == 1:
-                    act(out=ta[:], in_=sn[1][:], func=ACT.Copy, scale=sc[:, 1:2])
-                act(out=ph[k + 1][:], in_=sn[k][:], func=ACT.Identity, bias=uu[k][:], scale=nc0[:])
+
+        def chain_step(k):
+            act(out=sn[k][:], in_=ph[k][:], func=ACT.Sin)
+            act(out=cn[k][:], in_=ph[k][:], func=ACT.Sin, bias=0.5 * math.pi, scale=nsg[:])
+            act(out=uu[k][:], in_=cn[k][:], func=ACT.Identity, bias=ph[k][:], scale=s0)
+            act(out=ph[k + 1][:], in_=sn[k][:], func=ACT.Identity, bias=uu[k][:], scale=nc0[:])
+
+        def chain_end():
+            act(out=ta[:], in_=sn[1][:], func=ACT.Copy, scale=sc[:, 1:2])
             act(out=brad[:], in_=ps_p[:], func=ACT.Identity, bias=ph[2][:])
             act(out=amp[:], in_=cn[1][:], func=ACT.Identity, bias=ta[:], scale=sc[:, 0:1])
 
@@ -241,37 +258,40 @@ def tile_time2vec_kernel(tc, x, W, P, w, p, sine_w, cosine_w, out):
                     in_=o[:],
                 )
 
-        wpl = small("wpl", 2)
+        wpl = [small("wpl%d" % k, 2) for k in range(2)]
 
         def linear(i):
-            lin = work.tile([P128, 1024], F32, name="lin", tag="lin", bufs=4)
-            nc.gpsimd.tensor_scalar(
-                out=lin[:], in0=x_sb[i][:], scalar1=wpl[:, 0:1], scalar2=wpl[:, 1:2], op0=ALU.mult, op1=ALU.add
-            )
+            lin = work.tile([P128, 1024], F32, name="lin", tag="lin", bufs=8)
+            wp = wpl[0] if i < EARLY_LINEAR else wpl[1]
+            nc.gpsimd.tensor_scalar(out=lin[:], in0=x_sb[i][:], scalar1=wp[:, 0:1], scalar2=wp[:, 1:2], op0=ALU.mult, op1=ALU.add)
             nc.sync.dma_start(out=out[128 * i : 128 * (i + 1), 0:1024], in_=lin[:])
 
         interleave_w(0, 0)
         nc.vector.tensor_copy(out=sc[:], in_=scb[:, 0:64:16])
         interleave_w(1, 0)
         quantize_w(0, 0)
-        interleave_w(0, 1)
         quantize_w(1, 0)
-        interleave_w(1, 1)
-        quantize_w(0, 1)
-        quantize_w(1, 1)
-        chain()
+        chain_norm()
         for i in range(4):
             transpose_x(i)
+        parts = {1: chain_guess, 3: lambda: chain_step(0), 5: lambda: chain_step(1), 7: chain_end}
         for i in range(NT):
             copy_x(i)
+            if i in parts:
+                parts[i]()
             if i + 4 < NT:
                 transpose_x(i + 4)
             if i >= 1:
                 quantize_x(i - 1)
         quantize_x(NT - 1)
+        nc.vector.memset(gate[:], 1.0)
+        nc.vector.tensor_copy(out=wpl[0][:], in_=sc[:, 2:4])
         for u in range(4):
             matmuls(u)
-        nc.vector.tensor_copy(out=wpl[:], in_=sc[:, 2:4])
+        for i in range(EARLY_LINEAR):
+            linear(i)
+        interleave_w_gpsimd(0, 1)
+        interleave_w_gpsimd(1, 1)
 
         npieces = len(PIECES)
         paired = 10
@@ -280,8 +300,12 @@ def tile_time2vec_kernel(tc, x, W, P, w, p, sine_w, cosine_w, out):
             back_at.setdefault(2 * (k // 2) + 4 if k < paired else k + 3, []).append(k)
             out_at.setdefault(k + 4 if k < paired else k + 3, []).append(k)
         for u in range(4, 16):
-            mx_at.setdefault(2 * (u // 2) - 2, []).append(u)
+            mx_at.setdefault(max(2 * (u // 2) - 2, LATE_W_STEP if u >= 8 else 0), []).append(u)
         for s in range(npieces + 3):
+            if s == LATE_W_STEP:
+                quantize_w(0, 1)
+                quantize_w(1, 1)
+                nc.vector.tensor_copy(out=wpl[1][:], in_=sc[:, 2:4])
             if s < npieces:
                 whole_turns(s)
             if 1 <= s <= npieces:
@@ -294,5 +318,5 @@ def tile_time2vec_kernel(tc, x, W, P, w, p, sine_w, cosine_w, out):
                 sine(s - 1)
             for k in out_at.get(s, []):
                 scale_store(k)
-            if s < NT:
-                linear(s)
+            if EARLY_LINEAR <= s - LATE_W_STEP + EARLY_LINEAR < NT:
+                linear(s - LATE_W_STEP + EARLY_LINEAR)

@@ -22,11 +22,11 @@ INV_2PI = 1.0 / (2.0 * math.pi)
 GUESS = 0.68
 TINY = 1e-30
 GROUPS = ((0, 0), (1, 0), (0, 1), (1, 1))
-RUNS = (2, 2, 2, 2, 2, 2, 2, 1, 1)
+RUNS = (4, 4, 2, 2, 2, 1, 1)
 ON_VECTOR = (13, 15, 16)
-X_ON_VECTOR = (1, 3, 5, 7)
-EARLY_LINEAR = 2
-LATE_W_STEP = 7
+X_ON_VECTOR = (5, 7)
+WARM_ON_W = {(1, 0): 1, (0, 1): 2, (1, 1): 2}
+WARM_WITH_X = 6
 PIECES = [(u, 0, 4) for u in range(15)] + [(15, 0, 2), (15, 2, 4)]
 
 
@@ -67,10 +67,10 @@ def tile_time2vec_kernel(tc, x, W, P, w, p, sine_w, cosine_w, out):
 
         load_w(0, 0)
         load_w(1, 0)
-        for i in range(NT):
-            load_x(i)
         load_w(0, 1)
         load_w(1, 1)
+        for i in range(NT):
+            load_x(i)
 
         junk = small("junk")
         nc.scalar.activation(out=junk[:], in_=one[:], func=ACT.Abs_reciprocal_sqrt)
@@ -78,6 +78,14 @@ def tile_time2vec_kernel(tc, x, W, P, w, p, sine_w, cosine_w, out):
         nc.vector.tensor_copy(out=identb[:], in_=ident[:, 0:8])
         ps_p = psum.tile([P128, 8], F32, name="ps_p", tag="acc", bufs=4)
         nc.tensor.matmul(out=ps_p[:], lhsT=prow[:], rhs=identb[:], start=True, stop=True)
+        warm = psum.tile([P128, 512], F32, name="warm", tag="acc", bufs=4)
+
+        def keep_warm(g, h, j):
+            nc.tensor.matmul(out=warm[:], lhsT=prow[:], rhs=w_raw[g][h][:, j, :], start=True, stop=True)
+
+        for (g, h), count in WARM_ON_W.items():
+            for j in range(count):
+                keep_warm(g, h, j)
 
         wg = [[keep.tile([P128, 2048], BF16, name="wg%d%d" % (g, h), align_bytes=64) for h in range(2)] for g in range(2)]
         wq = [[keep.tile([P128, 512], U32, name="wq%d%d" % (g, h), align_bytes=64) for h in range(2)] for g in range(2)]
@@ -85,22 +93,11 @@ def tile_time2vec_kernel(tc, x, W, P, w, p, sine_w, cosine_w, out):
         xq = [[keep.tile([P128, 512], U32, name="xq%d%d" % (g, h), align_bytes=64) for h in range(2)] for g in range(2)]
         xs = [[keep.tile([P128, 512], U8, name="xs%d%d" % (g, h), align_bytes=64) for h in range(2)] for g in range(2)]
         st = {}
-        gate = small("gate")
 
         def interleave_w(g, h):
             nc.vector.tensor_copy(
                 out=wg[g][h][:].rearrange("p (c i j) -> p c j i", i=4, j=4),
                 in_=w_raw[g][h][:].rearrange("p j (c i) -> p c j i", i=4),
-            )
-
-        def interleave_w_gpsimd(g, h):
-            nc.gpsimd.tensor_scalar(
-                out=wg[g][h][:].rearrange("p (n j) -> p n j", j=4),
-                in0=w_raw[g][h][:].rearrange("p j n -> p n j"),
-                scalar1=gate[:],
-                scalar2=0.0,
-                op0=ALU.mult,
-                op1=ALU.add,
             )
 
         def quantize_w(g, h):
@@ -114,6 +111,8 @@ def tile_time2vec_kernel(tc, x, W, P, w, p, sine_w, cosine_w, out):
                 for u in range(2):
                     c = 2 * g + u
                     nc.tensor.transpose(xt[:, 128 * c : 128 * (c + 1)], words[:, 256 * g + u : 256 * (g + 1) : 2], ident[:])
+            if i < WARM_WITH_X:
+                keep_warm(0, 0, 0)
 
         def copy_x(i):
             xg = work.tile([P128, 1024], BF16, name="xg", tag="xg", bufs=8, align_bytes=64)
@@ -163,7 +162,7 @@ def tile_time2vec_kernel(tc, x, W, P, w, p, sine_w, cosine_w, out):
         swcw = scb[:, 0:32:16]
         act = nc.scalar.activation
 
-        def chain_norm():
+        def chain():
             act(out=ab[:], in_=swcw, func=ACT.Abs, bias=TINY, scale=0.5)
             act(out=dd[:], in_=ab[:, 0:1], func=ACT.Identity, bias=ab[:, 1:2])
             act(out=rs[:], in_=dd[:], func=ACT.Abs_reciprocal_sqrt)
@@ -173,8 +172,6 @@ def tile_time2vec_kernel(tc, x, W, P, w, p, sine_w, cosine_w, out):
             act(out=rr[:], in_=t2[:, 0:1], func=ACT.Abs_reciprocal_sqrt, bias=t2[:, 1:2])
             act(out=junk[:], in_=one[:], func=ACT.Sin)
             act(out=cs[:], in_=c1s1[:], func=ACT.Copy, scale=rr[:])
-
-        def chain_guess():
             act(out=sg[:], in_=s0, func=ACT.Sign, bias=TINY)
             act(out=hh[:], in_=c0, func=ACT.Identity, bias=0.5 * math.pi, scale=-0.5 * math.pi)
             act(out=m0[:], in_=c0, func=ACT.Copy, scale=s0)
@@ -182,15 +179,13 @@ def tile_time2vec_kernel(tc, x, W, P, w, p, sine_w, cosine_w, out):
             act(out=hs[:], in_=hh[:], func=ACT.Copy, scale=sg[:])
             act(out=nsg[:], in_=sg[:], func=ACT.Copy, scale=-1.0)
             act(out=ph[0][:], in_=m0[:], func=ACT.Identity, bias=hs[:], scale=GUESS)
-
-        def chain_step(k):
-            act(out=sn[k][:], in_=ph[k][:], func=ACT.Sin)
-            act(out=cn[k][:], in_=ph[k][:], func=ACT.Sin, bias=0.5 * math.pi, scale=nsg[:])
-            act(out=uu[k][:], in_=cn[k][:], func=ACT.Identity, bias=ph[k][:], scale=s0)
-            act(out=ph[k + 1][:], in_=sn[k][:], func=ACT.Identity, bias=uu[k][:], scale=nc0[:])
-
-        def chain_end():
-            act(out=ta[:], in_=sn[1][:], func=ACT.Copy, scale=sc[:, 1:2])
+            for k in range(2):
+                act(out=sn[k][:], in_=ph[k][:], func=ACT.Sin)
+                act(out=cn[k][:], in_=ph[k][:], func=ACT.Sin, bias=0.5 * math.pi, scale=nsg[:])
+                act(out=uu[k][:], in_=cn[k][:], func=ACT.Identity, bias=ph[k][:], scale=s0)
+                if k == 1:
+                    act(out=ta[:], in_=sn[1][:], func=ACT.Copy, scale=sc[:, 1:2])
+                act(out=ph[k + 1][:], in_=sn[k][:], func=ACT.Identity, bias=uu[k][:], scale=nc0[:])
             act(out=brad[:], in_=ps_p[:], func=ACT.Identity, bias=ph[2][:])
             act(out=amp[:], in_=cn[1][:], func=ACT.Identity, bias=ta[:], scale=sc[:, 0:1])
 
@@ -258,40 +253,37 @@ def tile_time2vec_kernel(tc, x, W, P, w, p, sine_w, cosine_w, out):
                     in_=o[:],
                 )
 
-        wpl = [small("wpl%d" % k, 2) for k in range(2)]
+        wpl = small("wpl", 2)
 
         def linear(i):
-            lin = work.tile([P128, 1024], F32, name="lin", tag="lin", bufs=8)
-            wp = wpl[0] if i < EARLY_LINEAR else wpl[1]
-            nc.gpsimd.tensor_scalar(out=lin[:], in0=x_sb[i][:], scalar1=wp[:, 0:1], scalar2=wp[:, 1:2], op0=ALU.mult, op1=ALU.add)
+            lin = work.tile([P128, 1024], F32, name="lin", tag="lin", bufs=4)
+            nc.gpsimd.tensor_scalar(
+                out=lin[:], in0=x_sb[i][:], scalar1=wpl[:, 0:1], scalar2=wpl[:, 1:2], op0=ALU.mult, op1=ALU.add
+            )
             nc.sync.dma_start(out=out[128 * i : 128 * (i + 1), 0:1024], in_=lin[:])
 
         interleave_w(0, 0)
         nc.vector.tensor_copy(out=sc[:], in_=scb[:, 0:64:16])
         interleave_w(1, 0)
         quantize_w(0, 0)
+        interleave_w(0, 1)
         quantize_w(1, 0)
-        chain_norm()
+        interleave_w(1, 1)
+        quantize_w(0, 1)
+        quantize_w(1, 1)
+        chain()
         for i in range(4):
             transpose_x(i)
-        parts = {1: chain_guess, 3: lambda: chain_step(0), 5: lambda: chain_step(1), 7: chain_end}
         for i in range(NT):
             copy_x(i)
-            if i in parts:
-                parts[i]()
             if i + 4 < NT:
                 transpose_x(i + 4)
             if i >= 1:
                 quantize_x(i - 1)
         quantize_x(NT - 1)
-        nc.vector.memset(gate[:], 1.0)
-        nc.vector.tensor_copy(out=wpl[0][:], in_=sc[:, 2:4])
         for u in range(4):
             matmuls(u)
-        for i in range(EARLY_LINEAR):
-            linear(i)
-        interleave_w_gpsimd(0, 1)
-        interleave_w_gpsimd(1, 1)
+        nc.vector.tensor_copy(out=wpl[:], in_=sc[:, 2:4])
 
         npieces = len(PIECES)
         paired = 10
@@ -300,12 +292,8 @@ def tile_time2vec_kernel(tc, x, W, P, w, p, sine_w, cosine_w, out):
             back_at.setdefault(2 * (k // 2) + 4 if k < paired else k + 3, []).append(k)
             out_at.setdefault(k + 4 if k < paired else k + 3, []).append(k)
         for u in range(4, 16):
-            mx_at.setdefault(max(2 * (u // 2) - 2, LATE_W_STEP if u >= 8 else 0), []).append(u)
+            mx_at.setdefault(2 * (u // 2) - 2, []).append(u)
         for s in range(npieces + 3):
-            if s == LATE_W_STEP:
-                quantize_w(0, 1)
-                quantize_w(1, 1)
-                nc.vector.tensor_copy(out=wpl[1][:], in_=sc[:, 2:4])
             if s < npieces:
                 whole_turns(s)
             if 1 <= s <= npieces:
@@ -318,5 +306,5 @@ def tile_time2vec_kernel(tc, x, W, P, w, p, sine_w, cosine_w, out):
                 sine(s - 1)
             for k in out_at.get(s, []):
                 scale_store(k)
-            if EARLY_LINEAR <= s - LATE_W_STEP + EARLY_LINEAR < NT:
-                linear(s - LATE_W_STEP + EARLY_LINEAR)
+            if s < NT:
+                linear(s)

@@ -27,6 +27,7 @@ ON_VECTOR = (13, 15, 16)
 X_ON_VECTOR = (5, 7)
 WARM_ON_W = {(1, 0): 1, (0, 1): 2, (1, 1): 2}
 WARM_WITH_X = 6
+LINEAR_ON_SCALAR = 2
 PIECES = [(u, 0, 4) for u in range(15)] + [(15, 0, 2), (15, 2, 4)]
 
 
@@ -257,9 +258,12 @@ def tile_time2vec_kernel(tc, x, W, P, w, p, sine_w, cosine_w, out):
 
         def linear(i):
             lin = work.tile([P128, 1024], F32, name="lin", tag="lin", bufs=4)
-            nc.gpsimd.tensor_scalar(
-                out=lin[:], in0=x_sb[i][:], scalar1=wpl[:, 0:1], scalar2=wpl[:, 1:2], op0=ALU.mult, op1=ALU.add
-            )
+            if i < LINEAR_ON_SCALAR:
+                act(out=lin[:], in_=x_sb[i][:], func=ACT.Identity, bias=sc[:, 3:4], scale=sc[:, 2:3])
+            else:
+                nc.gpsimd.tensor_scalar(
+                    out=lin[:], in0=x_sb[i][:], scalar1=wpl[:, 0:1], scalar2=wpl[:, 1:2], op0=ALU.mult, op1=ALU.add
+                )
             nc.sync.dma_start(out=out[128 * i : 128 * (i + 1), 0:1024], in_=lin[:])
 
         interleave_w(0, 0)
@@ -284,6 +288,8 @@ def tile_time2vec_kernel(tc, x, W, P, w, p, sine_w, cosine_w, out):
         for u in range(4):
             matmuls(u)
         nc.vector.tensor_copy(out=wpl[:], in_=sc[:, 2:4])
+        for i in range(LINEAR_ON_SCALAR):
+            linear(i)
 
         npieces = len(PIECES)
         paired = 10
@@ -306,5 +312,5 @@ def tile_time2vec_kernel(tc, x, W, P, w, p, sine_w, cosine_w, out):
                 sine(s - 1)
             for k in out_at.get(s, []):
                 scale_store(k)
-            if s < NT:
-                linear(s)
+            if s + LINEAR_ON_SCALAR < NT:
+                linear(s + LINEAR_ON_SCALAR)

@@ -23,7 +23,7 @@ GUESS = 0.68
 TINY = 1e-30
 GROUPS = ((0, 0), (1, 0), (0, 1), (1, 1))
 RUNS = (4, 4, 2, 2, 2, 1, 1)
-ON_VECTOR = (13, 15, 16)
+ON_VECTOR = (11, 13, 15, 16)
 X_ON_VECTOR = (5, 7)
 WARM_ON_W = {(1, 0): 1, (0, 1): 2, (1, 1): 2}
 WARM_WITH_X = 6

@@ -25,7 +25,7 @@ GROUPS = ((0, 0), (1, 0), (0, 1), (1, 1))
 RUNS = (4, 4, 2, 2, 2, 1, 1)
 ON_VECTOR = (11, 13, 15, 16)
 X_ON_VECTOR = (5, 7)
-WARM_ON_W = {(1, 0): 1, (0, 1): 2, (1, 1): 2}
+WARM_ON_W = {(0, 0): 1, (1, 0): 2, (1, 1): 2}
 WARM_WITH_X = 6
 LINEAR_ON_SCALAR = 2
 PIECES = [(u, 0, 4) for u in range(15)] + [(15, 0, 2), (15, 2, 4)]
@@ -52,24 +52,20 @@ def tile_time2vec_kernel(tc, x, W, P, w, p, sine_w, cosine_w, out):
         nc.vector.memset(one[:], 1.0)
         nc.vector.memset(prow[:], 0.0)
         make_identity(nc, ident[:])
-        nc.sync.dma_start(out=prow[0:8, :], in_=P.rearrange("(t q) -> t q", q=P128))
 
         x_sb = [keep.tile([P128, 1024], BF16, name="x_sb%d" % i) for i in range(NT)]
-        w_raw = [[keep.tile([P128, 4, 512], BF16, name="w_raw%d%d" % (g, h)) for h in range(2)] for g in range(2)]
+        w_all = [keep.tile([P128, 4, 1024], BF16, name="w_all%d" % g) for g in range(2)]
+        w_raw = [[w_all[g][:, :, 512 * h : 512 * (h + 1)] for h in range(2)] for g in range(2)]
 
         def load_x(i):
             nc.sync.dma_start(out=x_sb[i][:], in_=x[128 * i : 128 * (i + 1), :])
 
-        def load_w(g, h):
-            nc.sync.dma_start(
-                out=w_raw[g][h][:],
-                in_=W[512 * g : 512 * (g + 1), 512 * h : 512 * (h + 1)].rearrange("(p j) n -> p j n", j=4),
-            )
+        def load_w(g):
+            nc.sync.dma_start(out=w_all[g][:], in_=W[512 * g : 512 * (g + 1), :].rearrange("(p j) n -> p j n", j=4))
 
-        load_w(0, 0)
-        load_w(1, 0)
-        load_w(0, 1)
-        load_w(1, 1)
+        load_w(0)
+        nc.sync.dma_start(out=prow[0:8, :], in_=P.rearrange("(t q) -> t q", q=P128))
+        load_w(1)
         for i in range(NT):
             load_x(i)
 
@@ -98,7 +94,7 @@ def tile_time2vec_kernel(tc, x, W, P, w, p, sine_w, cosine_w, out):
         def interleave_w(g, h):
             nc.vector.tensor_copy(
                 out=wg[g][h][:].rearrange("p (c i j) -> p c j i", i=4, j=4),
-                in_=w_raw[g][h][:].rearrange("p j (c i) -> p c j i", i=4),
+                in_=w_raw[g][h].rearrange("p j (c i) -> p c j i", i=4),
             )
 
         def quantize_w(g, h):
@@ -268,12 +264,12 @@ def tile_time2vec_kernel(tc, x, W, P, w, p, sine_w, cosine_w, out):
 
         interleave_w(0, 0)
         nc.vector.tensor_copy(out=sc[:], in_=scb[:, 0:64:16])
-        interleave_w(1, 0)
-        quantize_w(0, 0)
         interleave_w(0, 1)
-        quantize_w(1, 0)
-        interleave_w(1, 1)
+        quantize_w(0, 0)
+        interleave_w(1, 0)
         quantize_w(0, 1)
+        interleave_w(1, 1)
+        quantize_w(1, 0)
         quantize_w(1, 1)
         chain()
         for i in range(4):

@@ -24,9 +24,10 @@ TINY = 1e-30
 GROUPS = ((0, 0), (1, 0), (0, 1), (1, 1))
 RUNS = (4, 4, 2, 2, 2, 1, 1)
 ON_VECTOR = (11, 13, 15, 16)
+OUT_LATE = (13,)
 X_ON_VECTOR = (5, 7)
 WARM_ON_W = {(0, 0): 1, (1, 0): 2, (1, 1): 2}
-WARM_WITH_X = 6
+WARM_WITH_X = 0
 LINEAR_ON_SCALAR = 2
 PIECES = [(u, 0, 4) for u in range(15)] + [(15, 0, 2), (15, 2, 4)]
 
@@ -292,7 +293,7 @@ def tile_time2vec_kernel(tc, x, W, P, w, p, sine_w, cosine_w, out):
         back_at, out_at, mx_at = {}, {}, {}
         for k in range(npieces):
             back_at.setdefault(2 * (k // 2) + 4 if k < paired else k + 3, []).append(k)
-            out_at.setdefault(k + 4 if k < paired else k + 3, []).append(k)
+            out_at.setdefault(k + 4 if k < paired or k in OUT_LATE else k + 3, []).append(k)
         for u in range(4, 16):
             mx_at.setdefault(2 * (u // 2) - 2, []).append(u)
         for s in range(npieces + 3):

@@ -26,8 +26,6 @@ RUNS = (4, 4, 2, 2, 2, 1, 1)
 ON_VECTOR = (11, 13, 15, 16)
 OUT_LATE = (13,)
 X_ON_VECTOR = (5, 7)
-WARM_ON_W = {(0, 0): 1, (1, 0): 2, (1, 1): 2}
-WARM_WITH_X = 0
 LINEAR_ON_SCALAR = 2
 PIECES = [(u, 0, 4) for u in range(15)] + [(15, 0, 2), (15, 2, 4)]
 
@@ -76,14 +74,6 @@ def tile_time2vec_kernel(tc, x, W, P, w, p, sine_w, cosine_w, out):
         nc.vector.tensor_copy(out=identb[:], in_=ident[:, 0:8])
         ps_p = psum.tile([P128, 8], F32, name="ps_p", tag="acc", bufs=4)
         nc.tensor.matmul(out=ps_p[:], lhsT=prow[:], rhs=identb[:], start=True, stop=True)
-        warm = psum.tile([P128, 512], F32, name="warm", tag="acc", bufs=4)
-
-        def keep_warm(g, h, j):
-            nc.tensor.matmul(out=warm[:], lhsT=prow[:], rhs=w_raw[g][h][:, j, :], start=True, stop=True)
-
-        for (g, h), count in WARM_ON_W.items():
-            for j in range(count):
-                keep_warm(g, h, j)
 
         wg = [[keep.tile([P128, 2048], BF16, name="wg%d%d" % (g, h), align_bytes=64) for h in range(2)] for g in range(2)]
         wq = [[keep.tile([P128, 512], U32, name="wq%d%d" % (g, h), align_bytes=64) for h in range(2)] for g in range(2)]
@@ -109,8 +99,6 @@ def tile_time2vec_kernel(tc, x, W, P, w, p, sine_w, cosine_w, out):
                 for u in range(2):
                     c = 2 * g + u
                     nc.tensor.transpose(xt[:, 128 * c : 128 * (c + 1)], words[:, 256 * g + u : 256 * (g + 1) : 2], ident[:])
-            if i < WARM_WITH_X:
-                keep_warm(0, 0, 0)
 
         def copy_x(i):
             xg = work.tile([P128, 1024], BF16, name="xg", tag="xg", bufs=8, align_bytes=64)

import math
from contextlib import ExitStack

import concourse.mybir as mybir
from concourse.masks import make_identity

FLOPS = 2 * 1024 * 1024 * 1024

F32 = mybir.dt.float32
BF16 = mybir.dt.bfloat16
I32 = mybir.dt.int32
U32 = mybir.dt.uint32
U8 = mybir.dt.uint8
E5X4 = mybir.dt.float8_e5m2_x4
ACT = mybir.ActivationFunctionType
ALU = mybir.AluOpType

P128 = 128
NT = 8
TWO_PI = 2.0 * math.pi
INV_2PI = 1.0 / (2.0 * math.pi)
GUESS = 0.68
TINY = 1e-30
GROUPS = ((0, 0), (1, 0), (0, 1), (1, 1))
RUNS = (4, 4, 2, 2, 2, 1, 1)
ON_VECTOR = (11, 13, 15, 16)
OUT_LATE = (13,)
X_ON_VECTOR = (5, 7)
LINEAR_ON_SCALAR = 2
PIECES = [(u, 0, 4) for u in range(15)] + [(15, 0, 2), (15, 2, 4)]


def tile_time2vec_kernel(tc, x, W, P, w, p, sine_w, cosine_w, out):
    nc = tc.nc
    with ExitStack() as ctx:
        keep = ctx.enter_context(tc.tile_pool(name="keep", bufs=1))
        work = ctx.enter_context(tc.tile_pool(name="work", bufs=3))
        psum = ctx.enter_context(tc.psum_pool(name="psum", bufs=4))
        ctx.enter_context(tc.manual_schedule())

        def small(name, n=1):
            return keep.tile([P128, n], F32, name=name)

        scb = keep.tile([P128, 64], BF16, name="scb")
        for col, src in enumerate((sine_w, cosine_w, w, p)):
            nc.sync.dma_start(out=scb[:, 16 * col : 16 * col + 1], in_=src.partition_broadcast(P128))
        one = small("one")
        prow = keep.tile([P128, P128], BF16, name="prow")
        ident = keep.tile([P128, P128], F32, name="ident")
        identb = keep.tile([P128, 8], BF16, name="identb")
        nc.vector.memset(one[:], 1.0)
        nc.vector.memset(prow[:], 0.0)
        make_identity(nc, ident[:])

        x_sb = [keep.tile([P128, 1024], BF16, name="x_sb%d" % i) for i in range(NT)]
        w_all = [keep.tile([P128, 4, 1024], BF16, name="w_all%d" % g) for g in range(2)]
        w_raw = [[w_all[g][:, :, 512 * h : 512 * (h + 1)] for h in range(2)] for g in range(2)]

        def load_x(i):
            nc.sync.dma_start(out=x_sb[i][:], in_=x[128 * i : 128 * (i + 1), :])

        def load_w(g):
            nc.sync.dma_start(out=w_all[g][:], in_=W[512 * g : 512 * (g + 1), :].rearrange("(p j) n -> p j n", j=4))

        load_w(0)
        nc.sync.dma_start(out=prow[0:8, :], in_=P.rearrange("(t q) -> t q", q=P128))
        load_w(1)
        for i in range(NT):
            load_x(i)

        junk = small("junk")
        nc.scalar.activation(out=junk[:], in_=one[:], func=ACT.Abs_reciprocal_sqrt)

        nc.vector.tensor_copy(out=identb[:], in_=ident[:, 0:8])
        ps_p = psum.tile([P128, 8], F32, name="ps_p", tag="acc", bufs=4)
        nc.tensor.matmul(out=ps_p[:], lhsT=prow[:], rhs=identb[:], start=True, stop=True)

        wg = [[keep.tile([P128, 2048], BF16, name="wg%d%d" % (g, h), align_bytes=64) for h in range(2)] for g in range(2)]
        wq = [[keep.tile([P128, 512], U32, name="wq%d%d" % (g, h), align_bytes=64) for h in range(2)] for g in range(2)]
        ws = [[keep.tile([P128, 512], U8, name="ws%d%d" % (g, h), align_bytes=64) for h in range(2)] for g in range(2)]
        xq = [[keep.tile([P128, 512], U32, name="xq%d%d" % (g, h), align_bytes=64) for h in range(2)] for g in range(2)]
        xs = [[keep.tile([P128, 512], U8, name="xs%d%d" % (g, h), align_bytes=64) for h in range(2)] for g in range(2)]
        st = {}

        def interleave_w(g, h):
            nc.vector.tensor_copy(
                out=wg[g][h][:].rearrange("p (c i j) -> p c j i", i=4, j=4),
                in_=w_raw[g][h].rearrange("p j (c i) -> p c j i", i=4),
            )

        def quantize_w(g, h):
            nc.vector.quantize_mx(out=wq[g][h][:].bitcast(E5X4), scales=ws[g][h][:], in_=wg[g][h][:])

        def transpose_x(i):
            xt = psum.tile([P128, 512], F32, name="xt", tag="tp", bufs=4)
            st["xt", i] = xt
            words = x_sb[i][:].bitcast(F32)
            for g in range(2):
                for u in range(2):
                    c = 2 * g + u
                    nc.tensor.transpose(xt[:, 128 * c : 128 * (c + 1)], words[:, 256 * g + u : 256 * (g + 1) : 2], ident[:])

        def copy_x(i):
            xg = work.tile([P128, 1024], BF16, name="xg", tag="xg", bufs=8, align_bytes=64)
            st["xg", i] = xg
            copy = nc.vector.tensor_copy if i in X_ON_VECTOR else nc.scalar.copy
            copy(
                out=xg[:].bitcast(F32).rearrange("p (g r u) -> p g r u", g=2, u=2),
                in_=st["xt", i][:].rearrange("p (g u r) -> p g r u", g=2, u=2),
            )

        def quantize_x(i):
            hb, iq = i // 4, i % 4
            for g in range(2):
                nc.vector.quantize_mx(
                    out=xq[g][hb][:, 128 * iq : 128 * (iq + 1)].bitcast(E5X4),
                    scales=xs[g][hb][:, 128 * iq : 128 * (iq + 1)],
                    in_=st["xg", i][:, 512 * g : 512 * (g + 1)],
                )

        def matmuls(u):
            hb, nh = GROUPS[u // 4]
            tq = u % 4
            acc = psum.tile([P128, 512], F32, name="acc", tag="acc", bufs=4)
            st["acc", u] = acc
            for g in range(2):
                nc.tensor.matmul_mx(
                    out=acc[:],
                    lhsT=wq[g][nh][:, 128 * tq : 128 * (tq + 1)].bitcast(E5X4),
                    lhsT_scale=ws[g][nh][:, 128 * tq : 128 * (tq + 1)],
                    rhs=xq[g][hb][:].bitcast(E5X4),
                    rhs_scale=xs[g][hb][:],
                    start=(g == 0),
                    stop=(g == 1),
                )

        sc = small("sc", 4)
        ab, c1s1, t2, cs = small("ab", 2), small("c1s1", 2), small("t2", 2), small("cs", 2)
        dd, rs, rd, rr = small("dd"), small("rs"), small("rd"), small("rr")
        sg, hh, m0, nsg, nc0, hs = small("sg"), small("hh"), small("m0"), small("nsg"), small("nc0"), small("hs")
        ph = [small("ph%d" % k) for k in range(3)]
        sn = [small("sn%d" % k) for k in range(2)]
        cn = [small("cn%d" % k) for k in range(2)]
        uu = [small("uu%d" % k) for k in range(2)]
        ta, amp = small("ta"), small("amp")
        brad = small("brad", 8)
        c0, s0 = cs[:, 0:1], cs[:, 1:2]
        swcw = scb[:, 0:32:16]
        act = nc.scalar.activation

        def chain():
            act(out=ab[:], in_=swcw, func=ACT.Abs, bias=TINY, scale=0.5)
            act(out=dd[:], in_=ab[:, 0:1], func=ACT.Identity, bias=ab[:, 1:2])
            act(out=rs[:], in_=dd[:], func=ACT.Abs_reciprocal_sqrt)
            act(out=rd[:], in_=rs[:], func=ACT.Square)
            act(out=t2[:], in_=swcw, func=ACT.Square, bias=1e-18, scale=rd[:])
            act(out=c1s1[:], in_=swcw, func=ACT.Copy, scale=rd[:])
            act(out=rr[:], in_=t2[:, 0:1], func=ACT.Abs_reciprocal_sqrt, bias=t2[:, 1:2])
            act(out=junk[:], in_=one[:], func=ACT.Sin)
            act(out=cs[:], in_=c1s1[:], func=ACT.Copy, scale=rr[:])
            act(out=sg[:], in_=s0, func=ACT.Sign, bias=TINY)
            act(out=hh[:], in_=c0, func=ACT.Identity, bias=0.5 * math.pi, scale=-0.5 * math.pi)
            act(out=m0[:], in_=c0, func=ACT.Copy, scale=s0)
            act(out=nc0[:], in_=c0, func=ACT.Copy, scale=-1.0)
            act(out=hs[:], in_=hh[:], func=ACT.Copy, scale=sg[:])
            act(out=nsg[:], in_=sg[:], func=ACT.Copy, scale=-1.0)
            act(out=ph[0][:], in_=m0[:], func=ACT.Identity, bias=hs[:], scale=GUESS)
            for k in range(2):
                act(out=sn[k][:], in_=ph[k][:], func=ACT.Sin)
                act(out=cn[k][:], in_=ph[k][:], func=ACT.Sin, bias=0.5 * math.pi, scale=nsg[:])
                act(out=uu[k][:], in_=cn[k][:], func=ACT.Identity, bias=ph[k][:], scale=s0)
                if k == 1:
                    act(out=ta[:], in_=sn[1][:], func=ACT.Copy, scale=sc[:, 1:2])
                act(out=ph[k + 1][:], in_=sn[k][:], func=ACT.Identity, bias=uu[k][:], scale=nc0[:])
            act(out=brad[:], in_=ps_p[:], func=ACT.Identity, bias=ph[2][:])
            act(out=amp[:], in_=cn[1][:], func=ACT.Identity, bias=ta[:], scale=sc[:, 0:1])

        def cols(k):
            u, b0, b1 = PIECES[k]
            return u, slice(128 * b0, 128 * b1), 128 * (b1 - b0)

        def whole_turns(k):
            u, cc, width = cols(k)
            t = 4 * GROUPS[u // 4][1] + u % 4
            n = work.tile([P128, width], I32, name="n", tag="n", bufs=3)
            st["n", k] = n
            nc.vector.tensor_scalar(
                out=n[:], in0=st["acc", u][:, cc], scalar1=brad[:, t : t + 1], scalar2=INV_2PI, op0=ALU.add, op1=ALU.mult
            )

        def fraction(k):
            u, cc, width = cols(k)
            f = work.tile([P128, width], F32, name="f", tag="f", bufs=3)
            st["f", k] = f
            nc.vector.scalar_tensor_tensor(
                out=f[:], in0=st["acc", u][:, cc], scalar=INV_2PI, in1=st["n", k][:], op0=ALU.mult, op1=ALU.subtract
            )

        def sine(k):
            u, cc, width = cols(k)
            t = 4 * GROUPS[u // 4][1] + u % 4
            s = work.tile([P128, width], F32, name="s", tag="s", bufs=5)
            st["s", k] = s
            act(out=s[:], in_=st["f", k][:], func=ACT.Sin, bias=brad[:, t : t + 1], scale=TWO_PI)

        def transpose_back(k):
            u, cc, width = cols(k)
            tp = psum.tile([P128, width], F32, name="tp", tag="tp", bufs=4)
            st["tp", k] = tp
            for b in range(width // 128):
                nc.tensor.transpose(tp[:, 128 * b : 128 * (b + 1)], st["s", k][:, 128 * b : 128 * (b + 1)], ident[:])

        run_of = {}
        first = 0
        for length in RUNS:
            for u in range(first, first + length):
                run_of[u] = (first, length)
            first += length

        def scale_store(k):
            u, b0, b1 = PIECES[k]
            first_u, length = run_of[u]
            nb = b1 - b0
            if ("o", first_u, b0) not in st:
                st["o", first_u, b0] = keep.tile([P128, nb, 128 * length], F32, name="o%d_%d" % (first_u, b0))
            o = st["o", first_u, b0]
            c = 128 * (u - first_u)
            banked = st["tp", k][:].rearrange("p (i n) -> p i n", n=128)
            if k in ON_VECTOR:
                nc.vector.tensor_scalar(out=o[:, :, c : c + 128], in0=banked, scalar1=amp[:], scalar2=None, op0=ALU.mult)
            else:
                act(out=o[:, :, c : c + 128], in_=banked, func=ACT.Copy, scale=amp[:])
            if u == first_u + length - 1:
                hb, nh = GROUPS[u // 4]
                r0 = 512 * hb + 128 * b0
                c0d = 1024 + 512 * nh + 128 * (first_u % 4)
                nc.sync.dma_start(
                    out=out[r0 : r0 + 128 * nb, c0d : c0d + 128 * length].rearrange("(i q) n -> q i n", q=P128),
                    in_=o[:],
                )

        wpl = small("wpl", 2)

        def linear(i):
            lin = work.tile([P128, 1024], F32, name="lin", tag="lin", bufs=4)
            if i < LINEAR_ON_SCALAR:
                act(out=lin[:], in_=x_sb[i][:], func=ACT.Identity, bias=sc[:, 3:4], scale=sc[:, 2:3])
            else:
                nc.gpsimd.tensor_scalar(
                    out=lin[:], in0=x_sb[i][:], scalar1=wpl[:, 0:1], scalar2=wpl[:, 1:2], op0=ALU.mult, op1=ALU.add
                )
            nc.sync.dma_start(out=out[128 * i : 128 * (i + 1), 0:1024], in_=lin[:])

        interleave_w(0, 0)
        nc.vector.tensor_copy(out=sc[:], in_=scb[:, 0:64:16])
        interleave_w(0, 1)
        quantize_w(0, 0)
        interleave_w(1, 0)
        quantize_w(0, 1)
        interleave_w(1, 1)
        quantize_w(1, 0)
        quantize_w(1, 1)
        chain()
        for i in range(4):
            transpose_x(i)
        for i in range(NT):
            copy_x(i)
            if i + 4 < NT:
                transpose_x(i + 4)
            if i >= 1:
                quantize_x(i - 1)
        quantize_x(NT - 1)
        for u in range(4):
            matmuls(u)
        nc.vector.tensor_copy(out=wpl[:], in_=sc[:, 2:4])
        for i in range(LINEAR_ON_SCALAR):
            linear(i)

        npieces = len(PIECES)
        paired = 10
        back_at, out_at, mx_at = {}, {}, {}
        for k in range(npieces):
            back_at.setdefault(2 * (k // 2) + 4 if k < paired else k + 3, []).append(k)
            out_at.setdefault(k + 4 if k < paired or k in OUT_LATE else k + 3, []).append(k)
        for u in range(4, 16):
            mx_at.setdefault(2 * (u // 2) - 2, []).append(u)
        for s in range(npieces + 3):
            if s < npieces:
                whole_turns(s)
            if 1 <= s <= npieces:
                fraction(s - 1)
            for k in back_at.get(s, []):
                transpose_back(k)
            for u in mx_at.get(s, []):
                matmuls(u)
            if 1 <= s <= npieces:
                sine(s - 1)
            for k in out_at.get(s, []):
                scale_store(k)
            if s + LINEAR_ON_SCALAR < NT:
                linear(s + LINEAR_ON_SCALAR)
